import numpy as np
import ml_dtypes


def mxq(x, axis, fmt="e4m3"):
    dtype, down = {"e4m3": (ml_dtypes.float8_e4m3fn, 7), "e5m2": (ml_dtypes.float8_e5m2, 14)}[fmt]
    v = np.moveaxis(np.asarray(x, np.float32).astype(ml_dtypes.bfloat16).astype(np.float64), axis, -1)
    blocks = v.reshape(v.shape[:-1] + (-1, 32))
    amax = np.abs(blocks).max(-1, keepdims=True)
    byte = np.maximum(np.where(amax > 0, np.frexp(amax)[1] - 1 + 127, 0) - down, 1)
    scale = np.exp2(byte - 127.0)
    codes = (blocks / scale).astype(np.float32).astype(dtype).astype(np.float64)
    return np.moveaxis((codes * scale).reshape(v.shape), -1, axis)


WIDE = False


def mx_kscale(k):
    if not WIDE:
        return np.ones(k)
    levels = np.array([10, -10, 5, -5, 0])
    a = np.random.permutation(np.resize(levels, k // 512 * 4)).reshape(k // 512, 4)
    idx = np.arange(k)
    return np.exp2(a[idx // 512, idx % 128 // 32])


BF16 = ml_dtypes.bfloat16


def bf(x):
    return np.asarray(x, np.float32).astype(BF16)


def f64(x):
    return np.asarray(x).astype(np.float64)


E2M1 = np.array([0.0, 0.5, 1.0, 1.5, 2.0, 3.0, 4.0, 6.0, -0.0, -0.5, -1.0, -1.5, -2.0, -3.0, -4.0, -6.0])


def pack_weight(w, fmt):
    k, n = w.shape
    w = f64(bf(w)).reshape(k // 32, 32, n)
    amax = np.abs(w).max(1)
    if fmt == "e4m3":
        byte = np.frexp(amax)[1] - 1 + 127 - 7
    else:
        mant, ex = np.frexp(amax / 6.0)
        byte = np.where(mant > 0.5, ex, ex - 1) + 127
    byte = np.clip(np.where(amax > 0, byte, 1), 1, 254)
    scaled = (w * np.exp2(127.0 - byte)[:, None, :]).reshape(k, n).astype(np.float32)
    by_word = np.ascontiguousarray(scaled.reshape(k // 512, 128, 4, n).transpose(0, 1, 3, 2))
    if fmt == "e4m3":
        words = by_word.astype(ml_dtypes.float8_e4m3fn).view(np.uint8)
    else:
        c = by_word.astype(ml_dtypes.float4_e2m1fn).view(np.uint8) & 0xF
        words = c[..., 0::2] | (c[..., 1::2] << 4)
    return np.ascontiguousarray(words), np.ascontiguousarray(byte.astype(np.uint8).reshape(k // 512, 16, n))


def unpack_weight(words, scales, fmt):
    g, p, n, _ = words.shape
    if fmt == "e4m3":
        vals = np.ascontiguousarray(words).view(ml_dtypes.float8_e4m3fn).astype(np.float64)
    else:
        nib = np.empty((g, p, n, 4), np.uint8)
        nib[..., 0::2] = words & 0xF
        nib[..., 1::2] = words >> 4
        vals = E2M1[nib]
    vals = vals * np.repeat(np.exp2(scales.astype(np.float64) - 127.0), 8, axis=1)[..., None]
    return vals.transpose(0, 1, 3, 2).reshape(g * 512, n)


N, C, D, H, W, NHEADS, KSIZE = 1, 3072, 2048, 16, 16, 8, 5
PAD = KSIZE // 2
HD = D // NHEADS
WIN = KSIZE * KSIZE
FMT = "e4m3"


def _patches(t):
    tp = np.pad(t, ((0, 0), (0, 0), (PAD, PAD), (PAD, PAD)))
    return np.stack([tp[:, :, i:i + H, j:j + W] for i in range(KSIZE) for j in range(KSIZE)], axis=2)


def setup_inputs():
    s = mx_kscale(C)
    a = np.sqrt(1.5) / HD ** 0.25
    g = np.concatenate([np.full(2 * D, a), np.ones(D)])
    x = bf(np.random.standard_normal((N, C, H, W)) * s[None, :, None, None])
    w = np.random.standard_normal((3 * D, C)) * g[:, None] / np.sqrt(C) / s[None, :]
    words, scales = pack_weight(np.ascontiguousarray(w.T), FMT)
    return {"x": x, "w_qkv_words": words, "w_qkv_scales": scales}


def reference(x, w_qkv_words, w_qkv_scales):
    xq = mxq(f64(x).reshape(N, C, H * W), 1, "e4m3")
    wq = unpack_weight(w_qkv_words, w_qkv_scales, FMT).T
    qkv = (wq @ xq).reshape(N, 3 * D, H, W)
    Q, K, V = np.split(qkv, 3, axis=1)
    Qh = Q.reshape(N, NHEADS, HD, 1, H, W)
    scores = np.sum(_patches(K).reshape(N, NHEADS, HD, WIN, H, W) * Qh, axis=2, keepdims=True)
    e = np.exp(scores - scores.max(axis=3, keepdims=True))
    att = e / e.sum(axis=3, keepdims=True)
    out = np.sum(_patches(V).reshape(N, NHEADS, HD, WIN, H, W) * att, axis=3).reshape(N, D, H, W)
    return out

@@ -1,0 +1,337 @@
+from contextlib import ExitStack
+
+import concourse.mybir as mybir
+from concourse.masks import make_identity
+
+F32 = mybir.dt.float32
+BF16 = mybir.dt.bfloat16
+I32 = mybir.dt.int32
+U32 = mybir.dt.uint32
+U8 = mybir.dt.uint8
+FP8X4 = mybir.dt.float8_e4m3fn_x4
+ALU = mybir.AluOpType
+FUNC = mybir.ActivationFunctionType
+AXIS = mybir.AxisListType
+
+P = 128
+PACK = 4
+C_IN = 3072
+PASSES = C_IN // (P * PACK)
+D = 2048
+HEADS = 8
+HEAD_DIM = D // HEADS
+SIDE = 16
+PIXELS = SIDE * SIDE
+REACH = 2
+WINDOW = (2 * REACH + 1) ** 2
+TILES = PIXELS // P
+TILE_ROWS = P // SIDE
+BAND_ROWS = TILE_ROWS + REACH
+BAND = BAND_ROWS * SIDE
+BAND_STEP = PIXELS - BAND
+OUTSIDE = WINDOW - (REACH + 1) ** 2
+PAIR = 2
+PAIR_DIM = PAIR * HEAD_DIM
+PLANES_PER_TILE = 4
+PLANE_SLOTS = 2
+BIG = 1.0e30
+
+FLOPS = 2 * 3 * D * C_IN * PIXELS + 2 * 2 * D * WINDOW * PIXELS
+
+
+def band(t):
+    return slice(BAND_STEP * t, BAND_STEP * t + BAND)
+
+
+def plane_rows(g):
+    return slice(PACK * (g % PLANES_PER_TILE), P)
+
+
+def plane_slot(g):
+    return g // PLANES_PER_TILE
+
+
+def tile_relation_w_kernel(tc, x, w_qkv_words, w_qkv_scales, out):
+    nc = tc.nc
+
+    x_rows = x[0].rearrange("(g p t) h w -> g p t (h w)", g=PASSES, p=P, t=PACK)
+    w_bytes = w_qkv_words.rearrange("g p n t -> p g (n t)")
+    out_rows = out[0].rearrange("(a p) h w -> p a (h w)", p=P)
+
+    with ExitStack() as stack:
+        stack.enter_context(tc.manual_schedule())
+        keep = stack.enter_context(tc.tile_pool(name="keep", bufs=1))
+
+        w_words = {}
+        for hp in range(HEADS // PAIR):
+            for s in range(3):
+                w_words[(hp, s)] = keep.tile(
+                    [P, PASSES, PAIR_DIM], U32, name="w_words_%d_%d" % (hp, s), align_bytes=64
+                )
+        w_planes = keep.tile([P, PLANE_SLOTS, 3 * D], U8, align_bytes=64)
+        x_words = keep.tile([P, PASSES, PIXELS], U32, align_bytes=64)
+        x_planes = keep.tile([P, PLANE_SLOTS, PIXELS], U8, align_bytes=64)
+        ident = keep.tile([P, P], F32)
+        cap = keep.tile([P, TILES, BAND], F32)
+        masked = [
+            keep.tile([P, TILES, BAND + OUTSIDE], F32, name="masked_%d" % i) for i in range(PAIR)
+        ]
+        att = [keep.tile([P, TILES, PIXELS], F32, name="att_%d" % i) for i in range(PAIR)]
+
+        nc.vector.memset(w_planes[:].bitcast(I32), 0)
+        for i in range(PAIR):
+            nc.vector.memset(att[i][:], 0.0)
+        make_identity(nc, ident[:])
+
+        with tc.tile_pool(name="setup", bufs=1) as setup:
+            x_raw = setup.tile([P, PASSES, PACK, PIXELS], BF16)
+            for g in range(PASSES):
+                nc.sync.dma_start(out=x_raw[:, g], in_=x_rows[g])
+            for slot in range(PLANE_SLOTS):
+                g_lo = slot * PLANES_PER_TILE
+                g_hi = min(g_lo + PLANES_PER_TILE, PASSES)
+                for quad in range(4):
+                    nc.sync.dma_start(
+                        out=w_planes[32 * quad : 32 * quad + PACK * (g_hi - g_lo), slot, :].bitcast(I32),
+                        in_=w_qkv_scales[g_lo:g_hi, PACK * quad : PACK * (quad + 1), :].bitcast(I32),
+                    )
+            for hp in range(HEADS // PAIR):
+                for s in range(3):
+                    first = s * D + hp * PAIR_DIM
+                    nc.sync.dma_start(
+                        out=w_words[(hp, s)][:].bitcast(I32),
+                        in_=w_bytes[:, :, PACK * first : PACK * (first + PAIR_DIM)].bitcast(I32),
+                    )
+
+            x_grouped = setup.tile([P, PASSES, PIXELS, PACK], BF16, align_bytes=64)
+            for g in range(PASSES):
+                nc.vector.tensor_copy(out=x_grouped[:, g], in_=x_raw[:, g].rearrange("p t n -> p n t"))
+                if g > 0:
+                    quantise_x(nc, x_grouped, x_words, x_planes, g - 1)
+            quantise_x(nc, x_grouped, x_words, x_planes, PASSES - 1)
+
+            build_mask(nc, setup, cap, masked)
+
+        qkv = stack.enter_context(tc.tile_pool(name="qkv", bufs=2))
+        work = stack.enter_context(tc.tile_pool(name="work", bufs=2))
+        small = stack.enter_context(tc.tile_pool(name="small", bufs=4))
+        ps_proj = stack.enter_context(tc.psum_pool(name="ps_proj", bufs=2))
+        ps_score = stack.enter_context(tc.psum_pool(name="ps_score", bufs=2))
+        ps_att_t = stack.enter_context(tc.psum_pool(name="ps_att_t", bufs=2))
+        ps_out = stack.enter_context(tc.psum_pool(name="ps_out", bufs=1))
+
+        def project_channel_major(hp, s, dest):
+            for half in range(2):
+                bank = ps_proj.tile([P, 2, PIXELS], F32, tag="proj")
+                for i in range(2):
+                    lo = P * (2 * half + i)
+                    first = s * D + hp * PAIR_DIM + lo
+                    for g in range(PASSES):
+                        nc.tensor.matmul_mx(
+                            out=bank[:, i, :],
+                            lhsT=w_words[(hp, s)][:, g, lo : lo + P].bitcast(FP8X4),
+                            lhsT_scale=w_planes[plane_rows(g), plane_slot(g), first : first + P],
+                            rhs=x_words[:, g, :].bitcast(FP8X4),
+                            rhs_scale=x_planes[plane_rows(g), plane_slot(g), :],
+                            start=(g == 0),
+                            stop=(g == PASSES - 1),
+                        )
+                nc.scalar.copy(out=dest[:, 2 * half : 2 * half + 2, :], in_=bank[:])
+
+        def project_pixel_major(hp, dest):
+            first = 2 * D + hp * PAIR_DIM
+            for t in range(TILES):
+                bank = ps_proj.tile([P, PAIR_DIM], F32, tag="proj")
+                pix = slice(P * t, P * (t + 1))
+                for g in range(PASSES):
+                    nc.tensor.matmul_mx(
+                        out=bank[:],
+                        lhsT=x_words[:, g, pix].bitcast(FP8X4),
+                        lhsT_scale=x_planes[plane_rows(g), plane_slot(g), pix],
+                        rhs=w_words[(hp, 2)][:, g, :].bitcast(FP8X4),
+                        rhs_scale=w_planes[plane_rows(g), plane_slot(g), first : first + PAIR_DIM],
+                        start=(g == 0),
+                        stop=(g == PASSES - 1),
+                    )
+                nc.scalar.copy(out=dest[:, t, :], in_=bank[:])
+
+        def attention_weights(q_sb, k_sb):
+            neg_max, total, exps = [], [], []
+            for i in range(PAIR):
+                score = ps_score.tile([P, TILES, BAND], F32, tag="score")
+                for t in range(TILES):
+                    for c in range(2):
+                        nc.tensor.matmul(
+                            out=score[:, t, :],
+                            lhsT=q_sb[:, 2 * i + c, P * t : P * (t + 1)],
+                            rhs=k_sb[:, 2 * i + c, band(t)],
+                            start=(c == 0),
+                            stop=(c == 1),
+                        )
+                nc.vector.tensor_tensor(
+                    out=masked[i][:, :, 0:BAND], in0=score[:], in1=cap[:], op=ALU.min
+                )
+                neg_max.append(small.tile([P, TILES], F32, name="neg_max_%d" % i, tag="neg_max"))
+                nc.vector.tensor_reduce(
+                    out=neg_max[i][:], in_=masked[i][:], axis=AXIS.X, op=ALU.max, negate=True
+                )
+            for i in range(PAIR):
+                total.append(small.tile([P, TILES], F32, name="total_%d" % i, tag="total"))
+                exps.append(
+                    work.tile([P, TILES, BAND + OUTSIDE], F32, name="exps_%d" % i, tag="exps")
+                )
+                for t in range(TILES):
+                    nc.scalar.activation(
+                        out=exps[i][:, t, :],
+                        in_=masked[i][:, t, :],
+                        func=FUNC.Exp,
+                        bias=neg_max[i][:, t : t + 1],
+                        scale=1.0,
+                        accum_out=total[i][:, t : t + 1],
+                    )
+            for i in range(PAIR):
+                inv_total = small.tile([P, TILES], F32, tag="inv_total")
+                nc.vector.reciprocal(out=inv_total[:], in_=total[i][:])
+                for t in range(TILES):
+                    nc.vector.tensor_scalar(
+                        out=att[i][:, t, band(t)],
+                        in0=exps[i][:, t, 0:BAND],
+                        scalar1=inv_total[:, t : t + 1],
+                        scalar2=None,
+                        op0=ALU.mult,
+                    )
+
+        def transpose_weights():
+            att_t = []
+            for i in range(PAIR):
+                bank = ps_att_t.tile([P, TILES, PIXELS], F32, tag="att_t")
+                for j in range(TILES):
+                    for t in range(TILES):
+                        nc.tensor.transpose(
+                            out=bank[:, j, P * t : P * (t + 1)],
+                            in_=att[i][:, t, P * j : P * (j + 1)],
+                            identity=ident[:],
+                        )
+                att_t.append(work.tile([P, TILES, PIXELS], F32, name="att_t_%d" % i, tag="att_t"))
+                nc.vector.tensor_copy(out=att_t[i][:], in_=bank[:])
+            return att_t
+
+        def weighted_sum(hp, v_sb, att_t):
+            for i in range(PAIR):
+                part = [
+                    ps_out.tile([P, 2, BAND], F32, name="part_%d" % j, tag="part_%d" % j)
+                    for j in range(TILES)
+                ]
+                for j in range(TILES):
+                    for c in range(2):
+                        chan = slice(HEAD_DIM * i + P * c, HEAD_DIM * i + P * (c + 1))
+                        nc.tensor.matmul(
+                            out=part[j][:, c, :],
+                            lhsT=v_sb[:, j, chan],
+                            rhs=att_t[i][:, j, band(j)],
+                            start=True,
+                            stop=True,
+                        )
+                res = work.tile([P, 2, PIXELS], F32, tag="res")
+                overlap = BAND - BAND_STEP
+                nc.vector.tensor_copy(out=res[:, :, 0:BAND], in_=part[0][:])
+                nc.vector.tensor_copy(out=res[:, :, BAND:PIXELS], in_=part[1][:, :, overlap:BAND])
+                nc.vector.tensor_tensor(
+                    out=res[:, :, BAND_STEP:BAND],
+                    in0=res[:, :, BAND_STEP:BAND],
+                    in1=part[1][:, :, 0:overlap],
+                    op=ALU.add,
+                )
+                head = PAIR * hp + i
+                nc.sync.dma_start(out=out_rows[:, 2 * head : 2 * head + 2, :], in_=res[:])
+
+        v_prev, att_t_prev = None, None
+        for hp in range(HEADS // PAIR):
+            if hp > 0:
+                att_t_prev = transpose_weights()
+            q_sb = qkv.tile([P, 2 * PAIR, PIXELS], F32, tag="q")
+            k_sb = qkv.tile([P, 2 * PAIR, PIXELS], F32, tag="k")
+            project_channel_major(hp, 0, q_sb)
+            project_channel_major(hp, 1, k_sb)
+            if hp > 0:
+                weighted_sum(hp - 1, v_prev, att_t_prev)
+            attention_weights(q_sb, k_sb)
+            v_sb = qkv.tile([P, TILES, PAIR_DIM], F32, tag="v")
+            project_pixel_major(hp, v_sb)
+            v_prev = v_sb
+        att_t_prev = transpose_weights()
+        weighted_sum(HEADS // PAIR - 1, v_prev, att_t_prev)
+
+
+def quantise_x(nc, x_grouped, x_words, x_planes, g):
+    nc.vector.quantize_mx(
+        out=x_words[:, g, :].bitcast(FP8X4),
+        scales=x_planes[plane_rows(g), plane_slot(g), :],
+        in_=x_grouped[:, g].rearrange("p n t -> p (n t)"),
+    )
+
+
+def build_mask(nc, pool, cap, masked):
+    pix = pool.tile([P, 1], I32)
+    nc.gpsimd.iota(pix[:], pattern=[[0, 1]], base=0, channel_multiplier=1)
+    pix_row = pool.tile([P, 1], I32)
+    nc.vector.tensor_single_scalar(out=pix_row[:], in_=pix[:], scalar=4, op=ALU.arith_shift_right)
+    pix_col = pool.tile([P, 1], I32)
+    nc.vector.tensor_single_scalar(out=pix_col[:], in_=pix[:], scalar=SIDE - 1, op=ALU.bitwise_and)
+    key_row = pool.tile([P, BAND_ROWS, SIDE], F32)
+    nc.gpsimd.iota(
+        key_row[:], pattern=[[1, BAND_ROWS], [0, SIDE]], base=0, channel_multiplier=0,
+        allow_small_or_imprecise_dtypes=True,
+    )
+    key_col = pool.tile([P, BAND_ROWS, SIDE], F32)
+    nc.gpsimd.iota(
+        key_col[:], pattern=[[0, BAND_ROWS], [1, SIDE]], base=0, channel_multiplier=0,
+        allow_small_or_imprecise_dtypes=True,
+    )
+    slot = pool.tile([P, OUTSIDE], F32)
+    nc.gpsimd.iota(
+        slot[:], pattern=[[1, OUTSIDE]], base=0, channel_multiplier=0,
+        allow_small_or_imprecise_dtypes=True,
+    )
+    neg_col = pool.tile([P, 1], F32)
+    nc.vector.tensor_scalar(
+        out=neg_col[:], in0=pix_col[:], scalar1=-1.0, scalar2=None, op0=ALU.mult
+    )
+    col_dist = pool.tile([P, BAND], F32)
+    nc.scalar.activation(
+        out=col_dist[:], in_=key_col[:].rearrange("p r c -> p (r c)"), func=FUNC.Square,
+        bias=neg_col[:, 0:1], scale=1.0,
+    )
+    far = pool.tile([P, TILES, BAND], F32)
+    for t in range(TILES):
+        neg_row = pool.tile([P, 1], F32, name="neg_row_%d" % t)
+        nc.vector.tensor_scalar(
+            out=neg_row[:], in0=pix_row[:], scalar1=-1.0, scalar2=-float(REACH * t),
+            op0=ALU.mult, op1=ALU.add,
+        )
+        row_dist = pool.tile([P, BAND], F32, name="row_dist_%d" % t)
+        nc.scalar.activation(
+            out=row_dist[:], in_=key_row[:].rearrange("p r c -> p (r c)"), func=FUNC.Square,
+            bias=neg_row[:, 0:1], scale=1.0,
+        )
+        nc.vector.tensor_tensor(out=far[:, t, :], in0=row_dist[:], in1=col_dist[:], op=ALU.max)
+    inside = pool.tile([P, TILES, BAND], F32)
+    nc.vector.tensor_scalar(
+        out=inside[:], in0=far[:], scalar1=REACH * REACH + 0.5, scalar2=None, op0=ALU.is_le
+    )
+    nc.vector.tensor_scalar(
+        out=cap[:], in0=inside[:], scalar1=2.0 * BIG, scalar2=-BIG, op0=ALU.mult, op1=ALU.add
+    )
+    count = pool.tile([P, TILES], F32)
+    nc.vector.tensor_reduce(out=count[:], in_=inside[:], axis=AXIS.X, op=ALU.add)
+    unused = pool.tile([P, TILES, OUTSIDE], F32)
+    for t in range(TILES):
+        nc.vector.tensor_scalar(
+            out=unused[:, t, :], in0=slot[:], scalar1=count[:, t : t + 1], scalar2=WINDOW - 0.5,
+            op0=ALU.add, op1=ALU.is_gt,
+        )
+    for tile_i in masked:
+        nc.vector.tensor_scalar(
+            out=tile_i[:, :, BAND : BAND + OUTSIDE], in0=unused[:], scalar1=-BIG, scalar2=None,
+            op0=ALU.mult,
+        )

@@ -97,11 +97,15 @@ def tile_relation_w_kernel(tc, x, w_qkv_words, w_qkv_scales, out):
                     )
             for hp in range(HEADS // PAIR):
                 for s in range(3):
-                    first = s * D + hp * PAIR_DIM
-                    nc.sync.dma_start(
-                        out=w_words[(hp, s)][:].bitcast(I32),
-                        in_=w_bytes[:, :, PACK * first : PACK * (first + PAIR_DIM)].bitcast(I32),
-                    )
+                    pieces = PAIR if (hp == 0 and s < 2) else 1
+                    width = PAIR_DIM // pieces
+                    for piece in range(pieces):
+                        lo = piece * width
+                        first = s * D + hp * PAIR_DIM + lo
+                        nc.sync.dma_start(
+                            out=w_words[(hp, s)][:, :, lo : lo + width].bitcast(I32),
+                            in_=w_bytes[:, :, PACK * first : PACK * (first + width)].bitcast(I32),
+                        )
 
             x_grouped = setup.tile([P, PASSES, PIXELS, PACK], BF16, align_bytes=64)
             for g in range(PASSES):
@@ -155,7 +159,7 @@ def tile_relation_w_kernel(tc, x, w_qkv_words, w_qkv_scales, out):
                     )
                 nc.scalar.copy(out=dest[:, t, :], in_=bank[:])
 
-        def attention_weights(q_sb, k_sb):
+        def scores_and_exps(q_sb, k_sb):
             neg_max, total, exps = [], [], []
             for i in range(PAIR):
                 score = ps_score.tile([P, TILES, BAND], F32, tag="score")
@@ -189,6 +193,9 @@ def tile_relation_w_kernel(tc, x, w_qkv_words, w_qkv_scales, out):
                         scale=1.0,
                         accum_out=total[i][:, t : t + 1],
                     )
+            return exps, total
+
+        def normalise(exps, total):
             for i in range(PAIR):
                 inv_total = small.tile([P, TILES], F32, tag="inv_total")
                 nc.vector.reciprocal(out=inv_total[:], in_=total[i][:])
@@ -245,22 +252,22 @@ def tile_relation_w_kernel(tc, x, w_qkv_words, w_qkv_scales, out):
                 head = PAIR * hp + i
                 nc.sync.dma_start(out=out_rows[:, 2 * head : 2 * head + 2, :], in_=res[:])
 
-        v_prev, att_t_prev = None, None
+        v_prev = None
         for hp in range(HEADS // PAIR):
-            if hp > 0:
-                att_t_prev = transpose_weights()
             q_sb = qkv.tile([P, 2 * PAIR, PIXELS], F32, tag="q")
             k_sb = qkv.tile([P, 2 * PAIR, PIXELS], F32, tag="k")
             project_channel_major(hp, 0, q_sb)
             project_channel_major(hp, 1, k_sb)
+            att_t = transpose_weights() if hp > 0 else None
+            exps, total = scores_and_exps(q_sb, k_sb)
             if hp > 0:
-                weighted_sum(hp - 1, v_prev, att_t_prev)
-            attention_weights(q_sb, k_sb)
+                weighted_sum(hp - 1, v_prev, att_t)
+            normalise(exps, total)
             v_sb = qkv.tile([P, TILES, PAIR_DIM], F32, tag="v")
             project_pixel_major(hp, v_sb)
             v_prev = v_sb
-        att_t_prev = transpose_weights()
-        weighted_sum(HEADS // PAIR - 1, v_prev, att_t_prev)
+        att_t = transpose_weights()
+        weighted_sum(HEADS // PAIR - 1, v_prev, att_t)
 
 
 def quantise_x(nc, x_grouped, x_words, x_planes, g):

@@ -83,29 +83,46 @@ def tile_relation_w_kernel(tc, x, w_qkv_words, w_qkv_scales, out):
             nc.vector.memset(att[i][:], 0.0)
         make_identity(nc, ident[:])
 
-        with tc.tile_pool(name="setup", bufs=1) as setup:
-            x_raw = setup.tile([P, PASSES, PACK, PIXELS], BF16)
-            for g in range(PASSES):
-                nc.sync.dma_start(out=x_raw[:, g], in_=x_rows[g])
+        def load_scales(s):
             for slot in range(PLANE_SLOTS):
                 g_lo = slot * PLANES_PER_TILE
                 g_hi = min(g_lo + PLANES_PER_TILE, PASSES)
                 for quad in range(4):
+                    rows = slice(32 * quad, 32 * quad + PACK * (g_hi - g_lo))
                     nc.sync.dma_start(
-                        out=w_planes[32 * quad : 32 * quad + PACK * (g_hi - g_lo), slot, :].bitcast(I32),
-                        in_=w_qkv_scales[g_lo:g_hi, PACK * quad : PACK * (quad + 1), :].bitcast(I32),
+                        out=w_planes[rows, slot, s * D : (s + 1) * D].bitcast(I32),
+                        in_=w_qkv_scales[
+                            g_lo:g_hi, PACK * quad : PACK * (quad + 1), s * D : (s + 1) * D
+                        ].bitcast(I32),
                     )
+
+        def load_words(hp, s):
+            first = s * D + hp * PAIR_DIM
+            if s == 2:
+                for g in range(PASSES):
+                    nc.sync.dma_start(
+                        out=w_words[(hp, s)][:, g, :].bitcast(I32),
+                        in_=w_bytes[:, g, PACK * first : PACK * (first + PAIR_DIM)].bitcast(I32),
+                    )
+            else:
+                pieces = PAIR if hp == 0 else 1
+                width = PAIR_DIM // pieces
+                for lo in range(0, PAIR_DIM, width):
+                    nc.sync.dma_start(
+                        out=w_words[(hp, s)][:, :, lo : lo + width].bitcast(I32),
+                        in_=w_bytes[:, :, PACK * (first + lo) : PACK * (first + lo + width)].bitcast(I32),
+                    )
+
+        mask_pool = stack.enter_context(tc.tile_pool(name="mask_pool", bufs=1))
+        with tc.tile_pool(name="setup", bufs=1) as setup:
+            x_raw = setup.tile([P, PASSES, PACK, PIXELS], BF16)
+            for g in range(PASSES):
+                nc.sync.dma_start(out=x_raw[:, g], in_=x_rows[g])
             for hp in range(HEADS // PAIR):
                 for s in range(3):
-                    pieces = PAIR if (hp == 0 and s < 2) else 1
-                    width = PAIR_DIM // pieces
-                    for piece in range(pieces):
-                        lo = piece * width
-                        first = s * D + hp * PAIR_DIM + lo
-                        nc.sync.dma_start(
-                            out=w_words[(hp, s)][:, :, lo : lo + width].bitcast(I32),
-                            in_=w_bytes[:, :, PACK * first : PACK * (first + width)].bitcast(I32),
-                        )
+                    if hp == 0:
+                        load_scales(s)
+                    load_words(hp, s)
 
             x_grouped = setup.tile([P, PASSES, PIXELS, PACK], BF16, align_bytes=64)
             for g in range(PASSES):
@@ -114,15 +131,15 @@ def tile_relation_w_kernel(tc, x, w_qkv_words, w_qkv_scales, out):
                     quantise_x(nc, x_grouped, x_words, x_planes, g - 1)
             quantise_x(nc, x_grouped, x_words, x_planes, PASSES - 1)
 
-            build_mask(nc, setup, cap, masked)
+        build_mask(nc, mask_pool, cap, masked)
 
         qkv = stack.enter_context(tc.tile_pool(name="qkv", bufs=2))
         work = stack.enter_context(tc.tile_pool(name="work", bufs=2))
         small = stack.enter_context(tc.tile_pool(name="small", bufs=4))
-        ps_proj = stack.enter_context(tc.psum_pool(name="ps_proj", bufs=2))
-        ps_score = stack.enter_context(tc.psum_pool(name="ps_score", bufs=2))
-        ps_att_t = stack.enter_context(tc.psum_pool(name="ps_att_t", bufs=2))
-        ps_out = stack.enter_context(tc.psum_pool(name="ps_out", bufs=1))
+        results = stack.enter_context(tc.tile_pool(name="results", bufs=HEADS))
+        ps_proj = stack.enter_context(tc.psum_pool(name="ps_proj", bufs=3))
+        ps_plain = stack.enter_context(tc.psum_pool(name="ps_plain", bufs=2))
+        ps_out = stack.enter_context(tc.psum_pool(name="ps_out", bufs=3))
 
         def project_channel_major(hp, s, dest):
             for half in range(2):
@@ -144,12 +161,14 @@ def tile_relation_w_kernel(tc, x, w_qkv_words, w_qkv_scales, out):
 
         def project_pixel_major(hp, dest):
             first = 2 * D + hp * PAIR_DIM
-            for t in range(TILES):
-                bank = ps_proj.tile([P, PAIR_DIM], F32, tag="proj")
-                pix = slice(P * t, P * (t + 1))
-                for g in range(PASSES):
+            banks = [
+                ps_proj.tile([P, PAIR_DIM], F32, name="v_bank_%d" % t, tag="proj") for t in range(TILES)
+            ]
+            for g in range(PASSES):
+                for t in range(TILES):
+                    pix = slice(P * t, P * (t + 1))
                     nc.tensor.matmul_mx(
-                        out=bank[:],
+                        out=banks[t][:],
                         lhsT=x_words[:, g, pix].bitcast(FP8X4),
                         lhsT_scale=x_planes[plane_rows(g), plane_slot(g), pix],
                         rhs=w_words[(hp, 2)][:, g, :].bitcast(FP8X4),
@@ -157,12 +176,13 @@ def tile_relation_w_kernel(tc, x, w_qkv_words, w_qkv_scales, out):
                         start=(g == 0),
                         stop=(g == PASSES - 1),
                     )
-                nc.scalar.copy(out=dest[:, t, :], in_=bank[:])
+            for t in range(TILES):
+                nc.scalar.copy(out=dest[:, t, :], in_=banks[t][:])
 
         def scores_and_exps(q_sb, k_sb):
             neg_max, total, exps = [], [], []
             for i in range(PAIR):
-                score = ps_score.tile([P, TILES, BAND], F32, tag="score")
+                score = ps_plain.tile([P, TILES, BAND], F32, tag="plain")
                 for t in range(TILES):
                     for c in range(2):
                         nc.tensor.matmul(
@@ -211,7 +231,7 @@ def tile_relation_w_kernel(tc, x, w_qkv_words, w_qkv_scales, out):
         def transpose_weights():
             att_t = []
             for i in range(PAIR):
-                bank = ps_att_t.tile([P, TILES, PIXELS], F32, tag="att_t")
+                bank = ps_plain.tile([P, TILES, PIXELS], F32, tag="plain")
                 for j in range(TILES):
                     for t in range(TILES):
                         nc.tensor.transpose(
@@ -220,13 +240,14 @@ def tile_relation_w_kernel(tc, x, w_qkv_words, w_qkv_scales, out):
                             identity=ident[:],
                         )
                 att_t.append(work.tile([P, TILES, PIXELS], F32, name="att_t_%d" % i, tag="att_t"))
-                nc.vector.tensor_copy(out=att_t[i][:], in_=bank[:])
+                for j in range(TILES):
+                    nc.vector.tensor_copy(out=att_t[i][:, j, band(j)], in_=bank[:, j, band(j)])
             return att_t
 
         def weighted_sum(hp, v_sb, att_t):
             for i in range(PAIR):
                 part = [
-                    ps_out.tile([P, 2, BAND], F32, name="part_%d" % j, tag="part_%d" % j)
+                    ps_out.tile([P, 2, BAND], F32, name="part_%d" % j, tag="part")
                     for j in range(TILES)
                 ]
                 for j in range(TILES):
@@ -239,10 +260,10 @@ def tile_relation_w_kernel(tc, x, w_qkv_words, w_qkv_scales, out):
                             start=True,
                             stop=True,
                         )
-                res = work.tile([P, 2, PIXELS], F32, tag="res")
+                res = results.tile([P, 2, PIXELS], F32, tag="res")
                 overlap = BAND - BAND_STEP
                 nc.vector.tensor_copy(out=res[:, :, 0:BAND], in_=part[0][:])
-                nc.vector.tensor_copy(out=res[:, :, BAND:PIXELS], in_=part[1][:, :, overlap:BAND])
+                nc.scalar.copy(out=res[:, :, BAND:PIXELS], in_=part[1][:, :, overlap:BAND])
                 nc.vector.tensor_tensor(
                     out=res[:, :, BAND_STEP:BAND],
                     in0=res[:, :, BAND_STEP:BAND],
@@ -252,22 +273,17 @@ def tile_relation_w_kernel(tc, x, w_qkv_words, w_qkv_scales, out):
                 head = PAIR * hp + i
                 nc.sync.dma_start(out=out_rows[:, 2 * head : 2 * head + 2, :], in_=res[:])
 
-        v_prev = None
         for hp in range(HEADS // PAIR):
             q_sb = qkv.tile([P, 2 * PAIR, PIXELS], F32, tag="q")
             k_sb = qkv.tile([P, 2 * PAIR, PIXELS], F32, tag="k")
             project_channel_major(hp, 0, q_sb)
             project_channel_major(hp, 1, k_sb)
-            att_t = transpose_weights() if hp > 0 else None
             exps, total = scores_and_exps(q_sb, k_sb)
-            if hp > 0:
-                weighted_sum(hp - 1, v_prev, att_t)
             normalise(exps, total)
             v_sb = qkv.tile([P, TILES, PAIR_DIM], F32, tag="v")
             project_pixel_major(hp, v_sb)
-            v_prev = v_sb
-        att_t = transpose_weights()
-        weighted_sum(HEADS // PAIR - 1, v_prev, att_t)
+            att_t = transpose_weights()
+            weighted_sum(hp, v_sb, att_t)
 
 
 def quantise_x(nc, x_grouped, x_words, x_planes, g):

@@ -118,9 +118,11 @@ def tile_relation_w_kernel(tc, x, w_qkv_words, w_qkv_scales, out):
             x_raw = setup.tile([P, PASSES, PACK, PIXELS], BF16)
             for g in range(PASSES):
                 nc.sync.dma_start(out=x_raw[:, g], in_=x_rows[g])
+            load_scales(0)
+            load_scales(1)
             for hp in range(HEADS // PAIR):
                 for s in range(3):
-                    if hp == 0:
+                    if hp == 0 and s == 2:
                         load_scales(s)
                     load_words(hp, s)
 

@@ -35,6 +35,7 @@ PAIR_DIM = PAIR * HEAD_DIM
 PLANES_PER_TILE = 4
 PLANE_SLOTS = 2
 BIG = 1.0e30
+PRODUCTS = ((0, 0), (0, 1), (1, 0))
 
 FLOPS = 2 * 3 * D * C_IN * PIXELS + 2 * 2 * D * WINDOW * PIXELS
 
@@ -143,6 +144,11 @@ def tile_relation_w_kernel(tc, x, w_qkv_words, w_qkv_scales, out):
         ps_plain = stack.enter_context(tc.psum_pool(name="ps_plain", bufs=2))
         ps_out = stack.enter_context(tc.psum_pool(name="ps_out", bufs=3))
 
+        def split(dest, where, bank):
+            hi, lo = dest
+            nc.scalar.copy(out=hi[where], in_=bank)
+            nc.vector.tensor_tensor(out=lo[where], in0=bank, in1=hi[where], op=ALU.subtract)
+
         def project_channel_major(hp, s, dest):
             for half in range(2):
                 bank = ps_proj.tile([P, 2, PIXELS], F32, tag="proj")
@@ -159,9 +165,9 @@ def tile_relation_w_kernel(tc, x, w_qkv_words, w_qkv_scales, out):
                             start=(g == 0),
                             stop=(g == PASSES - 1),
                         )
-                nc.scalar.copy(out=dest[:, 2 * half : 2 * half + 2, :], in_=bank[:])
+                split(dest, (slice(None), slice(2 * half, 2 * half + 2), slice(None)), bank[:])
 
-        def project_pixel_major(hp, dest):
+        def project_pixel_major(hp, dest, dest_f32):
             first = 2 * D + hp * PAIR_DIM
             banks = [
                 ps_proj.tile([P, PAIR_DIM], F32, name="v_bank_%d" % t, tag="proj") for t in range(TILES)
@@ -178,21 +184,25 @@ def tile_relation_w_kernel(tc, x, w_qkv_words, w_qkv_scales, out):
                         start=(g == 0),
                         stop=(g == PASSES - 1),
                     )
+            width = PAIR_DIM if dest_f32 is None else HEAD_DIM
             for t in range(TILES):
-                nc.scalar.copy(out=dest[:, t, :], in_=banks[t][:])
+                split(dest, (slice(None), t, slice(0, width)), banks[t][:, 0:width])
+                if dest_f32 is not None:
+                    nc.scalar.copy(out=dest_f32[:, t, :], in_=banks[t][:, width:PAIR_DIM])
 
-        def scores_and_exps(q_sb, k_sb):
+        def scores_and_exps(q, k):
             neg_max, total, exps = [], [], []
             for i in range(PAIR):
                 score = ps_plain.tile([P, TILES, BAND], F32, tag="plain")
                 for t in range(TILES):
-                    for c in range(2):
+                    terms = [(2 * i + c, u, v) for c in range(2) for u, v in PRODUCTS]
+                    for n, (c, u, v) in enumerate(terms):
                         nc.tensor.matmul(
                             out=score[:, t, :],
-                            lhsT=q_sb[:, 2 * i + c, P * t : P * (t + 1)],
-                            rhs=k_sb[:, 2 * i + c, band(t)],
-                            start=(c == 0),
-                            stop=(c == 1),
+                            lhsT=q[u][:, c, P * t : P * (t + 1)],
+                            rhs=k[v][:, c, band(t)],
+                            start=(n == 0),
+                            stop=(n == len(terms) - 1),
                         )
                 nc.vector.tensor_tensor(
                     out=masked[i][:, :, 0:BAND], in0=score[:], in1=cap[:], op=ALU.min
@@ -230,7 +240,7 @@ def tile_relation_w_kernel(tc, x, w_qkv_words, w_qkv_scales, out):
                         op0=ALU.mult,
                     )
 
-        def transpose_weights():
+        def transpose_weights(last):
             att_t = []
             for i in range(PAIR):
                 bank = ps_plain.tile([P, TILES, PIXELS], F32, tag="plain")
@@ -241,12 +251,22 @@ def tile_relation_w_kernel(tc, x, w_qkv_words, w_qkv_scales, out):
                             in_=att[i][:, t, P * j : P * (j + 1)],
                             identity=ident[:],
                         )
-                att_t.append(work.tile([P, TILES, PIXELS], F32, name="att_t_%d" % i, tag="att_t"))
-                for j in range(TILES):
-                    nc.vector.tensor_copy(out=att_t[i][:, j, band(j)], in_=bank[:, j, band(j)])
+                if last and i == PAIR - 1:
+                    whole = work.tile([P, TILES, PIXELS], F32, name="att_t_f32", tag="att_t_f32", bufs=1)
+                    for j in range(TILES):
+                        nc.vector.tensor_copy(out=whole[:, j, band(j)], in_=bank[:, j, band(j)])
+                    att_t.append([whole])
+                else:
+                    halves = [
+                        work.tile([P, TILES, PIXELS], BF16, name="att_t_%s_%d" % (h, i), tag="att_t_" + h)
+                        for h in ("hi", "lo")
+                    ]
+                    for j in range(TILES):
+                        split(halves, (slice(None), j, band(j)), bank[:, j, band(j)])
+                    att_t.append(halves)
             return att_t
 
-        def weighted_sum(hp, v_sb, att_t):
+        def weighted_sum(hp, v, v_f32, att_t):
             for i in range(PAIR):
                 part = [
                     ps_out.tile([P, 2, BAND], F32, name="part_%d" % j, tag="part")
@@ -255,13 +275,20 @@ def tile_relation_w_kernel(tc, x, w_qkv_words, w_qkv_scales, out):
                 for j in range(TILES):
                     for c in range(2):
                         chan = slice(HEAD_DIM * i + P * c, HEAD_DIM * i + P * (c + 1))
-                        nc.tensor.matmul(
-                            out=part[j][:, c, :],
-                            lhsT=v_sb[:, j, chan],
-                            rhs=att_t[i][:, j, band(j)],
-                            start=True,
-                            stop=True,
-                        )
+                        if len(att_t[i]) == 1:
+                            terms = [(v_f32[:, j, P * c : P * (c + 1)], att_t[i][0][:, j, band(j)])]
+                        else:
+                            terms = [
+                                (v[a][:, j, chan], att_t[i][b][:, j, band(j)]) for a, b in PRODUCTS
+                            ]
+                        for n, (lhs, rhs) in enumerate(terms):
+                            nc.tensor.matmul(
+                                out=part[j][:, c, :],
+                                lhsT=lhs,
+                                rhs=rhs,
+                                start=(n == 0),
+                                stop=(n == len(terms) - 1),
+                            )
                 res = results.tile([P, 2, PIXELS], F32, tag="res")
                 overlap = BAND - BAND_STEP
                 nc.vector.tensor_copy(out=res[:, :, 0:BAND], in_=part[0][:])
@@ -276,16 +303,20 @@ def tile_relation_w_kernel(tc, x, w_qkv_words, w_qkv_scales, out):
                 nc.sync.dma_start(out=out_rows[:, 2 * head : 2 * head + 2, :], in_=res[:])
 
         for hp in range(HEADS // PAIR):
-            q_sb = qkv.tile([P, 2 * PAIR, PIXELS], F32, tag="q")
-            k_sb = qkv.tile([P, 2 * PAIR, PIXELS], F32, tag="k")
-            project_channel_major(hp, 0, q_sb)
-            project_channel_major(hp, 1, k_sb)
-            exps, total = scores_and_exps(q_sb, k_sb)
+            last = hp == HEADS // PAIR - 1
+            q = [qkv.tile([P, 2 * PAIR, PIXELS], BF16, name="q_" + h, tag="q_" + h) for h in ("hi", "lo")]
+            k = [qkv.tile([P, 2 * PAIR, PIXELS], BF16, name="k_" + h, tag="k_" + h) for h in ("hi", "lo")]
+            project_channel_major(hp, 0, q)
+            project_channel_major(hp, 1, k)
+            exps, total = scores_and_exps(q, k)
             normalise(exps, total)
-            v_sb = qkv.tile([P, TILES, PAIR_DIM], F32, tag="v")
-            project_pixel_major(hp, v_sb)
-            att_t = transpose_weights()
-            weighted_sum(hp, v_sb, att_t)
+            v = [qkv.tile([P, TILES, PAIR_DIM], BF16, name="v_" + h, tag="v_" + h) for h in ("hi", "lo")]
+            v_f32 = None
+            if last:
+                v_f32 = qkv.tile([P, TILES, HEAD_DIM], F32, name="v_f32", tag="v_f32", bufs=1)
+            project_pixel_major(hp, v, v_f32)
+            att_t = transpose_weights(last)
+            weighted_sum(hp, v, v_f32, att_t)
 
 
 def quantise_x(nc, x_grouped, x_words, x_planes, g):

@@ -32,8 +32,6 @@ BAND_STEP = PIXELS - BAND
 OUTSIDE = WINDOW - (REACH + 1) ** 2
 PAIR = 2
 PAIR_DIM = PAIR * HEAD_DIM
-PLANES_PER_TILE = 4
-PLANE_SLOTS = 2
 BIG = 1.0e30
 PRODUCTS = ((0, 0), (0, 1), (1, 0))
 
@@ -44,163 +42,165 @@ def band(t):
     return slice(BAND_STEP * t, BAND_STEP * t + BAND)
 
 
-def plane_rows(g):
-    return slice(PACK * (g % PLANES_PER_TILE), P)
-
-
-def plane_slot(g):
-    return g // PLANES_PER_TILE
-
-
 def tile_relation_w_kernel(tc, x, w_qkv_words, w_qkv_scales, out):
     nc = tc.nc
+    pairs = HEADS // PAIR
 
-    x_rows = x[0].rearrange("(g p t) h w -> g p t (h w)", g=PASSES, p=P, t=PACK)
+    x_rows = x[0].rearrange("(g p t) h w -> p g t (h w)", g=PASSES, p=P, t=PACK)
     w_bytes = w_qkv_words.rearrange("g p n t -> p g (n t)")
+    w_scale_rows = w_qkv_scales.rearrange("g (q r) n -> q r g n", q=4)
     out_rows = out[0].rearrange("(a p) h w -> p a (h w)", p=P)
 
     with ExitStack() as stack:
         stack.enter_context(tc.manual_schedule())
         keep = stack.enter_context(tc.tile_pool(name="keep", bufs=1))
 
-        w_words = {}
-        for hp in range(HEADS // PAIR):
-            for s in range(3):
-                w_words[(hp, s)] = keep.tile(
-                    [P, PASSES, PAIR_DIM], U32, name="w_words_%d_%d" % (hp, s), align_bytes=64
-                )
-        w_planes = keep.tile([P, PLANE_SLOTS, 3 * D], U8, align_bytes=64)
+        w_words = [
+            [
+                keep.tile([P, PASSES, PAIR_DIM], U32, name="w_words_%d_%d" % (b, s), align_bytes=64)
+                for s in range(3)
+            ]
+            for b in range(2)
+        ]
+        w_planes = [
+            keep.tile([P, PASSES, 3, PAIR_DIM], U8, name="w_planes_%d" % b, align_bytes=64)
+            for b in range(2)
+        ]
         x_words = keep.tile([P, PASSES, PIXELS], U32, align_bytes=64)
-        x_planes = keep.tile([P, PLANE_SLOTS, PIXELS], U8, align_bytes=64)
+        x_planes = keep.tile([P, PASSES, PIXELS], U8, align_bytes=64)
         ident = keep.tile([P, P], F32)
         cap = keep.tile([P, TILES, BAND], F32)
         masked = [
             keep.tile([P, TILES, BAND + OUTSIDE], F32, name="masked_%d" % i) for i in range(PAIR)
         ]
         att = [keep.tile([P, TILES, PIXELS], F32, name="att_%d" % i) for i in range(PAIR)]
+        warm = keep.tile([P, 1], F32)
 
-        nc.vector.memset(w_planes[:].bitcast(I32), 0)
-        for i in range(PAIR):
-            nc.vector.memset(att[i][:], 0.0)
-        make_identity(nc, ident[:])
+        def clear_planes(engine, b, s):
+            engine.memset(w_planes[b][:, :, s, :].bitcast(I32), 0)
 
-        def load_scales(s):
-            for slot in range(PLANE_SLOTS):
-                g_lo = slot * PLANES_PER_TILE
-                g_hi = min(g_lo + PLANES_PER_TILE, PASSES)
-                for quad in range(4):
-                    rows = slice(32 * quad, 32 * quad + PACK * (g_hi - g_lo))
-                    nc.sync.dma_start(
-                        out=w_planes[rows, slot, s * D : (s + 1) * D].bitcast(I32),
-                        in_=w_qkv_scales[
-                            g_lo:g_hi, PACK * quad : PACK * (quad + 1), s * D : (s + 1) * D
-                        ].bitcast(I32),
-                    )
+        clear_planes(nc.vector, 0, 0)
+        clear_planes(nc.gpsimd, 0, 1)
+        clear_planes(nc.gpsimd, 0, 2)
+        nc.vector.memset(warm[:], 0.0)
+        nc.scalar.activation(out=warm[:], in_=warm[:], func=FUNC.Exp)
 
-        def load_words(hp, s):
+        def load_scales(hp, s):
             first = s * D + hp * PAIR_DIM
-            if s == 2:
-                for g in range(PASSES):
-                    nc.sync.dma_start(
-                        out=w_words[(hp, s)][:, g, :].bitcast(I32),
-                        in_=w_bytes[:, g, PACK * first : PACK * (first + PAIR_DIM)].bitcast(I32),
-                    )
-            else:
-                pieces = PAIR if hp == 0 else 1
-                width = PAIR_DIM // pieces
-                for lo in range(0, PAIR_DIM, width):
-                    nc.sync.dma_start(
-                        out=w_words[(hp, s)][:, :, lo : lo + width].bitcast(I32),
-                        in_=w_bytes[:, :, PACK * (first + lo) : PACK * (first + lo + width)].bitcast(I32),
-                    )
+            for quad in range(4):
+                nc.sync.dma_start(
+                    out=w_planes[hp % 2][32 * quad : 32 * quad + PACK, :, s, :].bitcast(I32),
+                    in_=w_scale_rows[quad, :, :, first : first + PAIR_DIM].bitcast(I32),
+                )
+
+        def load_words(hp, s, pieces=1):
+            first = s * D + hp * PAIR_DIM
+            width = PAIR_DIM // pieces
+            for lo in range(0, PAIR_DIM, width):
+                nc.sync.dma_start(
+                    out=w_words[hp % 2][s][:, :, lo : lo + width].bitcast(I32),
+                    in_=w_bytes[:, :, PACK * (first + lo) : PACK * (first + lo + width)].bitcast(I32),
+                )
 
         mask_pool = stack.enter_context(tc.tile_pool(name="mask_pool", bufs=1))
         with tc.tile_pool(name="setup", bufs=1) as setup:
             x_raw = setup.tile([P, PASSES, PACK, PIXELS], BF16)
-            for g in range(PASSES):
-                nc.sync.dma_start(out=x_raw[:, g], in_=x_rows[g])
-            load_scales(0)
-            load_scales(1)
-            for hp in range(HEADS // PAIR):
-                for s in range(3):
-                    if hp == 0 and s == 2:
-                        load_scales(s)
-                    load_words(hp, s)
+            for g in range(0, PASSES, 2):
+                nc.sync.dma_start(out=x_raw[:, g : g + 2], in_=x_rows[:, g : g + 2])
+                if g == 2:
+                    load_scales(0, 0)
+            load_words(0, 0, pieces=2)
+            for s in (1, 2):
+                load_scales(0, s)
+                load_words(0, s)
+
+            build_mask(nc, mask_pool, cap, masked)
+            make_identity(nc, ident[:])
+            for i in range(PAIR):
+                nc.gpsimd.memset(att[i][:], 0.0)
+            for s in range(3):
+                clear_planes(nc.gpsimd, 1, s)
 
             x_grouped = setup.tile([P, PASSES, PIXELS, PACK], BF16, align_bytes=64)
             for g in range(PASSES):
-                nc.vector.tensor_copy(out=x_grouped[:, g], in_=x_raw[:, g].rearrange("p t n -> p n t"))
+                rows = x_raw[:, g].rearrange("p t n -> p n t")
+                half = PIXELS // 2
+                nc.scalar.copy(out=x_grouped[:, g, 0:half, :], in_=rows[:, 0:half, :])
+                nc.vector.tensor_copy(out=x_grouped[:, g, half:PIXELS, :], in_=rows[:, half:PIXELS, :])
                 if g > 0:
                     quantise_x(nc, x_grouped, x_words, x_planes, g - 1)
             quantise_x(nc, x_grouped, x_words, x_planes, PASSES - 1)
 
-        build_mask(nc, mask_pool, cap, masked)
+        def load_pair(hp):
+            for s in range(3):
+                load_scales(hp, s)
+                load_words(hp, s)
+
+        load_pair(1)
 
         qkv = stack.enter_context(tc.tile_pool(name="qkv", bufs=2))
         work = stack.enter_context(tc.tile_pool(name="work", bufs=2))
         small = stack.enter_context(tc.tile_pool(name="small", bufs=4))
         results = stack.enter_context(tc.tile_pool(name="results", bufs=HEADS))
         ps_proj = stack.enter_context(tc.psum_pool(name="ps_proj", bufs=3))
-        ps_plain = stack.enter_context(tc.psum_pool(name="ps_plain", bufs=2))
-        ps_out = stack.enter_context(tc.psum_pool(name="ps_out", bufs=3))
+        ps_att = stack.enter_context(tc.psum_pool(name="ps_att", bufs=5))
+
+        q, k, v, v_f32, att_t = {}, {}, {}, {}, {}
+
+        def halves(pool, shape, name):
+            return [pool.tile(shape, BF16, name=name + h, tag=name + h) for h in ("_hi", "_lo")]
 
         def split(dest, where, bank):
             hi, lo = dest
             nc.scalar.copy(out=hi[where], in_=bank)
             nc.vector.tensor_tensor(out=lo[where], in0=bank, in1=hi[where], op=ALU.subtract)
 
-        def project_channel_major(hp, s, dest):
-            for half in range(2):
-                bank = ps_proj.tile([P, 2, PIXELS], F32, tag="proj")
-                for i in range(2):
-                    lo = P * (2 * half + i)
-                    first = s * D + hp * PAIR_DIM + lo
-                    for g in range(PASSES):
-                        nc.tensor.matmul_mx(
-                            out=bank[:, i, :],
-                            lhsT=w_words[(hp, s)][:, g, lo : lo + P].bitcast(FP8X4),
-                            lhsT_scale=w_planes[plane_rows(g), plane_slot(g), first : first + P],
-                            rhs=x_words[:, g, :].bitcast(FP8X4),
-                            rhs_scale=x_planes[plane_rows(g), plane_slot(g), :],
-                            start=(g == 0),
-                            stop=(g == PASSES - 1),
-                        )
-                split(dest, (slice(None), slice(2 * half, 2 * half + 2), slice(None)), bank[:])
-
-        def project_pixel_major(hp, dest, dest_f32):
-            first = 2 * D + hp * PAIR_DIM
-            banks = [
-                ps_proj.tile([P, PAIR_DIM], F32, name="v_bank_%d" % t, tag="proj") for t in range(TILES)
-            ]
-            for g in range(PASSES):
-                for t in range(TILES):
-                    pix = slice(P * t, P * (t + 1))
+        def project_channel_major(hp, s, half):
+            dest = (q, k)[s][hp]
+            bank = ps_proj.tile([P, 2, PIXELS], F32, tag="proj")
+            for i in range(2):
+                lo = P * (2 * half + i)
+                for g in range(PASSES):
                     nc.tensor.matmul_mx(
-                        out=banks[t][:],
-                        lhsT=x_words[:, g, pix].bitcast(FP8X4),
-                        lhsT_scale=x_planes[plane_rows(g), plane_slot(g), pix],
-                        rhs=w_words[(hp, 2)][:, g, :].bitcast(FP8X4),
-                        rhs_scale=w_planes[plane_rows(g), plane_slot(g), first : first + PAIR_DIM],
+                        out=bank[:, i, :],
+                        lhsT=w_words[hp % 2][s][:, g, lo : lo + P].bitcast(FP8X4),
+                        lhsT_scale=w_planes[hp % 2][:, g, s, lo : lo + P],
+                        rhs=x_words[:, g, :].bitcast(FP8X4),
+                        rhs_scale=x_planes[:, g, :],
                         start=(g == 0),
                         stop=(g == PASSES - 1),
                     )
-            width = PAIR_DIM if dest_f32 is None else HEAD_DIM
-            for t in range(TILES):
-                split(dest, (slice(None), t, slice(0, width)), banks[t][:, 0:width])
-                if dest_f32 is not None:
-                    nc.scalar.copy(out=dest_f32[:, t, :], in_=banks[t][:, width:PAIR_DIM])
+            split(dest, (slice(None), slice(2 * half, 2 * half + 2), slice(None)), bank[:])
 
-        def scores_and_exps(q, k):
+        def project_pixel_major(hp, t):
+            bank = ps_proj.tile([P, PAIR_DIM], F32, name="v_bank", tag="proj")
+            pix = slice(P * t, P * (t + 1))
+            for g in range(PASSES):
+                nc.tensor.matmul_mx(
+                    out=bank[:],
+                    lhsT=x_words[:, g, pix].bitcast(FP8X4),
+                    lhsT_scale=x_planes[:, g, pix],
+                    rhs=w_words[hp % 2][2][:, g, :].bitcast(FP8X4),
+                    rhs_scale=w_planes[hp % 2][:, g, 2, :],
+                    start=(g == 0),
+                    stop=(g == PASSES - 1),
+                )
+            width = PAIR_DIM if v_f32[hp] is None else HEAD_DIM
+            split(v[hp], (slice(None), t, slice(0, width)), bank[:, 0:width])
+            if v_f32[hp] is not None:
+                nc.scalar.copy(out=v_f32[hp][:, t, :], in_=bank[:, width:PAIR_DIM])
+
+        def scores_and_weights(hp):
             neg_max, total, exps = [], [], []
             for i in range(PAIR):
-                score = ps_plain.tile([P, TILES, BAND], F32, tag="plain")
+                score = ps_att.tile([P, TILES, BAND], F32, tag="att")
                 for t in range(TILES):
-                    terms = [(2 * i + c, u, v) for c in range(2) for u, v in PRODUCTS]
-                    for n, (c, u, v) in enumerate(terms):
+                    terms = [(2 * i + c, a, b) for a, b in PRODUCTS for c in range(2)]
+                    for n, (c, a, b) in enumerate(terms):
                         nc.tensor.matmul(
                             out=score[:, t, :],
-                            lhsT=q[u][:, c, P * t : P * (t + 1)],
-                            rhs=k[v][:, c, band(t)],
+                            lhsT=q[hp][a][:, c, P * t : P * (t + 1)],
+                            rhs=k[hp][b][:, c, band(t)],
                             start=(n == 0),
                             stop=(n == len(terms) - 1),
                         )
@@ -225,9 +225,6 @@ def tile_relation_w_kernel(tc, x, w_qkv_words, w_qkv_scales, out):
                         scale=1.0,
                         accum_out=total[i][:, t : t + 1],
                     )
-            return exps, total
-
-        def normalise(exps, total):
             for i in range(PAIR):
                 inv_total = small.tile([P, TILES], F32, tag="inv_total")
                 nc.vector.reciprocal(out=inv_total[:], in_=total[i][:])
@@ -240,10 +237,10 @@ def tile_relation_w_kernel(tc, x, w_qkv_words, w_qkv_scales, out):
                         op0=ALU.mult,
                     )
 
-        def transpose_weights(last):
-            att_t = []
+        def transpose_weights(hp):
+            att_t[hp] = []
             for i in range(PAIR):
-                bank = ps_plain.tile([P, TILES, PIXELS], F32, tag="plain")
+                bank = ps_att.tile([P, TILES, PIXELS], F32, tag="att")
                 for j in range(TILES):
                     for t in range(TILES):
                         nc.tensor.transpose(
@@ -251,35 +248,32 @@ def tile_relation_w_kernel(tc, x, w_qkv_words, w_qkv_scales, out):
                             in_=att[i][:, t, P * j : P * (j + 1)],
                             identity=ident[:],
                         )
-                if last and i == PAIR - 1:
+                if v_f32[hp] is not None and i == PAIR - 1:
                     whole = work.tile([P, TILES, PIXELS], F32, name="att_t_f32", tag="att_t_f32", bufs=1)
                     for j in range(TILES):
                         nc.vector.tensor_copy(out=whole[:, j, band(j)], in_=bank[:, j, band(j)])
-                    att_t.append([whole])
+                    att_t[hp].append([whole])
                 else:
-                    halves = [
-                        work.tile([P, TILES, PIXELS], BF16, name="att_t_%s_%d" % (h, i), tag="att_t_" + h)
-                        for h in ("hi", "lo")
-                    ]
+                    pieces = halves(work, [P, TILES, PIXELS], "att_t")
                     for j in range(TILES):
-                        split(halves, (slice(None), j, band(j)), bank[:, j, band(j)])
-                    att_t.append(halves)
-            return att_t
+                        split(pieces, (slice(None), j, band(j)), bank[:, j, band(j)])
+                    att_t[hp].append(pieces)
 
-        def weighted_sum(hp, v, v_f32, att_t):
+        def weighted_sum(hp):
             for i in range(PAIR):
                 part = [
-                    ps_out.tile([P, 2, BAND], F32, name="part_%d" % j, tag="part")
+                    ps_att.tile([P, 2, BAND], F32, name="part_%d" % j, tag="att")
                     for j in range(TILES)
                 ]
+                weights = att_t[hp][i]
                 for j in range(TILES):
                     for c in range(2):
-                        chan = slice(HEAD_DIM * i + P * c, HEAD_DIM * i + P * (c + 1))
-                        if len(att_t[i]) == 1:
-                            terms = [(v_f32[:, j, P * c : P * (c + 1)], att_t[i][0][:, j, band(j)])]
+                        if len(weights) == 1:
+                            terms = [(v_f32[hp][:, j, P * c : P * (c + 1)], weights[0][:, j, band(j)])]
                         else:
+                            chan = slice(HEAD_DIM * i + P * c, HEAD_DIM * i + P * (c + 1))
                             terms = [
-                                (v[a][:, j, chan], att_t[i][b][:, j, band(j)]) for a, b in PRODUCTS
+                                (v[hp][a][:, j, chan], weights[b][:, j, band(j)]) for a, b in PRODUCTS
                             ]
                         for n, (lhs, rhs) in enumerate(terms):
                             nc.tensor.matmul(
@@ -302,27 +296,34 @@ def tile_relation_w_kernel(tc, x, w_qkv_words, w_qkv_scales, out):
                 head = PAIR * hp + i
                 nc.sync.dma_start(out=out_rows[:, 2 * head : 2 * head + 2, :], in_=res[:])
 
-        for hp in range(HEADS // PAIR):
-            last = hp == HEADS // PAIR - 1
-            q = [qkv.tile([P, 2 * PAIR, PIXELS], BF16, name="q_" + h, tag="q_" + h) for h in ("hi", "lo")]
-            k = [qkv.tile([P, 2 * PAIR, PIXELS], BF16, name="k_" + h, tag="k_" + h) for h in ("hi", "lo")]
-            project_channel_major(hp, 0, q)
-            project_channel_major(hp, 1, k)
-            exps, total = scores_and_exps(q, k)
-            normalise(exps, total)
-            v = [qkv.tile([P, TILES, PAIR_DIM], BF16, name="v_" + h, tag="v_" + h) for h in ("hi", "lo")]
-            v_f32 = None
-            if last:
-                v_f32 = qkv.tile([P, TILES, HEAD_DIM], F32, name="v_f32", tag="v_f32", bufs=1)
-            project_pixel_major(hp, v, v_f32)
-            att_t = transpose_weights(last)
-            weighted_sum(hp, v, v_f32, att_t)
+        for hp in range(pairs):
+            q[hp] = halves(qkv, [P, 2 * PAIR, PIXELS], "q")
+            k[hp] = halves(qkv, [P, 2 * PAIR, PIXELS], "k")
+            v[hp] = halves(qkv, [P, TILES, PAIR_DIM], "v")
+            v_f32[hp] = None
+            if hp == pairs - 1:
+                v_f32[hp] = qkv.tile([P, TILES, HEAD_DIM], F32, name="v_f32", tag="v_f32", bufs=1)
+            project_channel_major(hp, 0, 0)
+            if hp == 1:
+                transpose_weights(0)
+            project_channel_major(hp, 0, 1)
+            project_channel_major(hp, 1, 0)
+            project_channel_major(hp, 1, 1)
+            project_pixel_major(hp, 0)
+            scores_and_weights(hp)
+            project_pixel_major(hp, 1)
+            if hp + 2 < pairs:
+                load_pair(hp + 2)
+            if hp > 0:
+                weighted_sum(hp - 1)
+                transpose_weights(hp)
+        weighted_sum(pairs - 1)
 
 
 def quantise_x(nc, x_grouped, x_words, x_planes, g):
     nc.vector.quantize_mx(
         out=x_words[:, g, :].bitcast(FP8X4),
-        scales=x_planes[plane_rows(g), plane_slot(g), :],
+        scales=x_planes[:, g, :],
         in_=x_grouped[:, g].rearrange("p n t -> p (n t)"),
     )
 

@@ -63,8 +63,18 @@ def tile_relation_w_kernel(tc, x, w_qkv_words, w_qkv_scales, out):
             for b in range(2)
         ]
         w_planes = [
-            keep.tile([P, PASSES, 3, PAIR_DIM], U8, name="w_planes_%d" % b, align_bytes=64)
+            [
+                keep.tile([P, PASSES, PAIR_DIM], U8, name="w_planes_%d_%d" % (b, s), align_bytes=64)
+                for s in range(3)
+            ]
             for b in range(2)
+        ]
+        first_words = [
+            [
+                keep.tile([P, PASSES, HEAD_DIM], U32, name="first_words_%d_%d" % (s, i), align_bytes=64)
+                for i in range(PAIR)
+            ]
+            for s in range(2)
         ]
         x_words = keep.tile([P, PASSES, PIXELS], U32, align_bytes=64)
         x_planes = keep.tile([P, PASSES, PIXELS], U8, align_bytes=64)
@@ -77,7 +87,7 @@ def tile_relation_w_kernel(tc, x, w_qkv_words, w_qkv_scales, out):
         warm = keep.tile([P, 1], F32)
 
         def clear_planes(engine, b, s):
-            engine.memset(w_planes[b][:, :, s, :].bitcast(I32), 0)
+            engine.memset(w_planes[b][s][:].bitcast(I32), 0)
 
         clear_planes(nc.vector, 0, 0)
         clear_planes(nc.gpsimd, 0, 1)
@@ -89,18 +99,21 @@ def tile_relation_w_kernel(tc, x, w_qkv_words, w_qkv_scales, out):
             first = s * D + hp * PAIR_DIM
             for quad in range(4):
                 nc.sync.dma_start(
-                    out=w_planes[hp % 2][32 * quad : 32 * quad + PACK, :, s, :].bitcast(I32),
+                    out=w_planes[hp % 2][s][32 * quad : 32 * quad + PACK].bitcast(I32),
                     in_=w_scale_rows[quad, :, :, first : first + PAIR_DIM].bitcast(I32),
                 )
 
-        def load_words(hp, s, pieces=1):
-            first = s * D + hp * PAIR_DIM
-            width = PAIR_DIM // pieces
-            for lo in range(0, PAIR_DIM, width):
-                nc.sync.dma_start(
-                    out=w_words[hp % 2][s][:, :, lo : lo + width].bitcast(I32),
-                    in_=w_bytes[:, :, PACK * (first + lo) : PACK * (first + lo + width)].bitcast(I32),
-                )
+        def load_words(tile, first, passes=slice(0, PASSES)):
+            width = tile.shape[2]
+            nc.sync.dma_start(
+                out=tile[:, passes, :].bitcast(I32),
+                in_=w_bytes[:, passes, PACK * first : PACK * (first + width)].bitcast(I32),
+            )
+
+        def load_pair(hp):
+            for s in range(3):
+                load_scales(hp, s)
+                load_words(w_words[hp % 2][s], s * D + hp * PAIR_DIM)
 
         mask_pool = stack.enter_context(tc.tile_pool(name="mask_pool", bufs=1))
         with tc.tile_pool(name="setup", bufs=1) as setup:
@@ -109,33 +122,32 @@ def tile_relation_w_kernel(tc, x, w_qkv_words, w_qkv_scales, out):
                 nc.sync.dma_start(out=x_raw[:, g : g + 2], in_=x_rows[:, g : g + 2])
                 if g == 2:
                     load_scales(0, 0)
-            load_words(0, 0, pieces=2)
-            for s in (1, 2):
-                load_scales(0, s)
-                load_words(0, s)
+            for i in range(PAIR):
+                load_words(first_words[0][i], HEAD_DIM * i)
+            load_scales(0, 1)
+            for i in range(PAIR):
+                load_words(first_words[1][i], D + HEAD_DIM * i)
+            load_scales(0, 2)
+            half = PASSES // 2
+            load_words(w_words[0][2], 2 * D, slice(0, half))
+            load_words(w_words[0][2], 2 * D, slice(half, PASSES))
 
             build_mask(nc, mask_pool, cap, masked)
             make_identity(nc, ident[:])
-            for i in range(PAIR):
-                nc.gpsimd.memset(att[i][:], 0.0)
-            for s in range(3):
-                clear_planes(nc.gpsimd, 1, s)
 
             x_grouped = setup.tile([P, PASSES, PIXELS, PACK], BF16, align_bytes=64)
             for g in range(PASSES):
                 rows = x_raw[:, g].rearrange("p t n -> p n t")
-                half = PIXELS // 2
-                nc.scalar.copy(out=x_grouped[:, g, 0:half, :], in_=rows[:, 0:half, :])
-                nc.vector.tensor_copy(out=x_grouped[:, g, half:PIXELS, :], in_=rows[:, half:PIXELS, :])
+                nc.scalar.copy(out=x_grouped[:, g, 0:P, :], in_=rows[:, 0:P, :])
+                nc.vector.tensor_copy(out=x_grouped[:, g, P:PIXELS, :], in_=rows[:, P:PIXELS, :])
                 if g > 0:
                     quantise_x(nc, x_grouped, x_words, x_planes, g - 1)
             quantise_x(nc, x_grouped, x_words, x_planes, PASSES - 1)
 
-        def load_pair(hp):
-            for s in range(3):
-                load_scales(hp, s)
-                load_words(hp, s)
-
+        for s in range(3):
+            clear_planes(nc.vector, 1, s)
+        for i in range(PAIR):
+            nc.vector.memset(att[i][:], 0.0)
         load_pair(1)
 
         qkv = stack.enter_context(tc.tile_pool(name="qkv", bufs=2))
@@ -145,7 +157,10 @@ def tile_relation_w_kernel(tc, x, w_qkv_words, w_qkv_scales, out):
         ps_proj = stack.enter_context(tc.psum_pool(name="ps_proj", bufs=3))
         ps_att = stack.enter_context(tc.psum_pool(name="ps_att", bufs=5))
 
-        q, k, v, v_f32, att_t = {}, {}, {}, {}, {}
+        q, k, v, att_t = {}, {}, {}, {}
+        whole = [
+            qkv.tile([P, 2, PIXELS], F32, name="whole_%d" % s, tag="whole_%d" % s, bufs=1) for s in range(2)
+        ]
 
         def halves(pool, shape, name):
             return [pool.tile(shape, BF16, name=name + h, tag=name + h) for h in ("_hi", "_lo")]
@@ -155,168 +170,152 @@ def tile_relation_w_kernel(tc, x, w_qkv_words, w_qkv_scales, out):
             nc.scalar.copy(out=hi[where], in_=bank)
             nc.vector.tensor_tensor(out=lo[where], in0=bank, in1=hi[where], op=ALU.subtract)
 
-        def project_channel_major(hp, s, half):
-            dest = (q, k)[s][hp]
+        def project_channel_major(hp, s, i):
             bank = ps_proj.tile([P, 2, PIXELS], F32, tag="proj")
-            for i in range(2):
-                lo = P * (2 * half + i)
+            for c in range(2):
+                lo = P * c if hp == 0 else HEAD_DIM * i + P * c
+                words = first_words[s][i] if hp == 0 else w_words[hp % 2][s]
+                plane_lo = HEAD_DIM * i + P * c
                 for g in range(PASSES):
                     nc.tensor.matmul_mx(
-                        out=bank[:, i, :],
-                        lhsT=w_words[hp % 2][s][:, g, lo : lo + P].bitcast(FP8X4),
-                        lhsT_scale=w_planes[hp % 2][:, g, s, lo : lo + P],
+                        out=bank[:, c, :],
+                        lhsT=words[:, g, lo : lo + P].bitcast(FP8X4),
+                        lhsT_scale=w_planes[hp % 2][s][:, g, plane_lo : plane_lo + P],
                         rhs=x_words[:, g, :].bitcast(FP8X4),
                         rhs_scale=x_planes[:, g, :],
                         start=(g == 0),
                         stop=(g == PASSES - 1),
                     )
-            split(dest, (slice(None), slice(2 * half, 2 * half + 2), slice(None)), bank[:])
+            if hp == 0 and i == 0:
+                nc.scalar.copy(out=whole[s][:], in_=bank[:])
+            else:
+                split((q, k)[s][hp], (slice(None), slice(2 * i, 2 * i + 2), slice(None)), bank[:])
 
-        def project_pixel_major(hp, t):
-            bank = ps_proj.tile([P, PAIR_DIM], F32, name="v_bank", tag="proj")
-            pix = slice(P * t, P * (t + 1))
+        def project_pixel_major(hp, tiles):
+            banks = {}
+            for t in tiles:
+                banks[t] = ps_proj.tile([P, PAIR_DIM], F32, name="v_bank_%d" % t, tag="proj")
             for g in range(PASSES):
-                nc.tensor.matmul_mx(
-                    out=bank[:],
-                    lhsT=x_words[:, g, pix].bitcast(FP8X4),
-                    lhsT_scale=x_planes[:, g, pix],
-                    rhs=w_words[hp % 2][2][:, g, :].bitcast(FP8X4),
-                    rhs_scale=w_planes[hp % 2][:, g, 2, :],
-                    start=(g == 0),
-                    stop=(g == PASSES - 1),
-                )
-            width = PAIR_DIM if v_f32[hp] is None else HEAD_DIM
-            split(v[hp], (slice(None), t, slice(0, width)), bank[:, 0:width])
-            if v_f32[hp] is not None:
-                nc.scalar.copy(out=v_f32[hp][:, t, :], in_=bank[:, width:PAIR_DIM])
-
-        def scores_and_weights(hp):
-            neg_max, total, exps = [], [], []
-            for i in range(PAIR):
-                score = ps_att.tile([P, TILES, BAND], F32, tag="att")
-                for t in range(TILES):
-                    terms = [(2 * i + c, a, b) for a, b in PRODUCTS for c in range(2)]
-                    for n, (c, a, b) in enumerate(terms):
-                        nc.tensor.matmul(
-                            out=score[:, t, :],
-                            lhsT=q[hp][a][:, c, P * t : P * (t + 1)],
-                            rhs=k[hp][b][:, c, band(t)],
-                            start=(n == 0),
-                            stop=(n == len(terms) - 1),
-                        )
-                nc.vector.tensor_tensor(
-                    out=masked[i][:, :, 0:BAND], in0=score[:], in1=cap[:], op=ALU.min
-                )
-                neg_max.append(small.tile([P, TILES], F32, name="neg_max_%d" % i, tag="neg_max"))
-                nc.vector.tensor_reduce(
-                    out=neg_max[i][:], in_=masked[i][:], axis=AXIS.X, op=ALU.max, negate=True
-                )
-            for i in range(PAIR):
-                total.append(small.tile([P, TILES], F32, name="total_%d" % i, tag="total"))
-                exps.append(
-                    work.tile([P, TILES, BAND + OUTSIDE], F32, name="exps_%d" % i, tag="exps")
-                )
-                for t in range(TILES):
-                    nc.scalar.activation(
-                        out=exps[i][:, t, :],
-                        in_=masked[i][:, t, :],
-                        func=FUNC.Exp,
-                        bias=neg_max[i][:, t : t + 1],
-                        scale=1.0,
-                        accum_out=total[i][:, t : t + 1],
+                for t in tiles:
+                    pix = slice(P * t, P * (t + 1))
+                    nc.tensor.matmul_mx(
+                        out=banks[t][:],
+                        lhsT=x_words[:, g, pix].bitcast(FP8X4),
+                        lhsT_scale=x_planes[:, g, pix],
+                        rhs=w_words[hp % 2][2][:, g, :].bitcast(FP8X4),
+                        rhs_scale=w_planes[hp % 2][2][:, g, :],
+                        start=(g == 0),
+                        stop=(g == PASSES - 1),
                     )
-            for i in range(PAIR):
-                inv_total = small.tile([P, TILES], F32, tag="inv_total")
-                nc.vector.reciprocal(out=inv_total[:], in_=total[i][:])
-                for t in range(TILES):
-                    nc.vector.tensor_scalar(
-                        out=att[i][:, t, band(t)],
-                        in0=exps[i][:, t, 0:BAND],
-                        scalar1=inv_total[:, t : t + 1],
-                        scalar2=None,
-                        op0=ALU.mult,
-                    )
+            for t in tiles:
+                split(v[hp], (slice(None), t, slice(None)), banks[t][:])
 
-        def transpose_weights(hp):
-            att_t[hp] = []
-            for i in range(PAIR):
-                bank = ps_att.tile([P, TILES, PIXELS], F32, tag="att")
-                for j in range(TILES):
-                    for t in range(TILES):
-                        nc.tensor.transpose(
-                            out=bank[:, j, P * t : P * (t + 1)],
-                            in_=att[i][:, t, P * j : P * (j + 1)],
-                            identity=ident[:],
-                        )
-                if v_f32[hp] is not None and i == PAIR - 1:
-                    whole = work.tile([P, TILES, PIXELS], F32, name="att_t_f32", tag="att_t_f32", bufs=1)
-                    for j in range(TILES):
-                        nc.vector.tensor_copy(out=whole[:, j, band(j)], in_=bank[:, j, band(j)])
-                    att_t[hp].append([whole])
+        def scores(hp, i):
+            score = ps_att.tile([P, TILES, BAND], F32, tag="att")
+            for t in range(TILES):
+                pix = slice(P * t, P * (t + 1))
+                if hp == 0 and i == 0:
+                    terms = [(whole[0][:, c, pix], whole[1][:, c, band(t)]) for c in range(2)]
                 else:
-                    pieces = halves(work, [P, TILES, PIXELS], "att_t")
-                    for j in range(TILES):
-                        split(pieces, (slice(None), j, band(j)), bank[:, j, band(j)])
-                    att_t[hp].append(pieces)
+                    terms = [
+                        (q[hp][a][:, 2 * i + c, pix], k[hp][b][:, 2 * i + c, band(t)])
+                        for a, b in PRODUCTS
+                        for c in range(2)
+                    ]
+                for n, (lhs, rhs) in enumerate(terms):
+                    nc.tensor.matmul(
+                        out=score[:, t, :], lhsT=lhs, rhs=rhs, start=(n == 0), stop=(n == len(terms) - 1)
+                    )
+            nc.vector.tensor_tensor(out=masked[i][:, :, 0:BAND], in0=score[:], in1=cap[:], op=ALU.min)
+            neg_max = small.tile([P, TILES], F32, tag="neg_max")
+            nc.vector.tensor_reduce(
+                out=neg_max[:], in_=masked[i][:], axis=AXIS.X, op=ALU.max, negate=True
+            )
+            total = small.tile([P, TILES], F32, tag="total")
+            exps = work.tile([P, TILES, BAND + OUTSIDE], F32, tag="exps")
+            for t in range(TILES):
+                nc.scalar.activation(
+                    out=exps[:, t, :],
+                    in_=masked[i][:, t, :],
+                    func=FUNC.Exp,
+                    bias=neg_max[:, t : t + 1],
+                    scale=1.0,
+                    accum_out=total[:, t : t + 1],
+                )
+            inv_total = small.tile([P, TILES], F32, tag="inv_total")
+            nc.vector.reciprocal(out=inv_total[:], in_=total[:])
+            for t in range(TILES):
+                nc.vector.tensor_scalar(
+                    out=att[i][:, t, band(t)],
+                    in0=exps[:, t, 0:BAND],
+                    scalar1=inv_total[:, t : t + 1],
+                    scalar2=None,
+                    op0=ALU.mult,
+                )
+
+        def transpose_weights(hp, i):
+            bank = ps_att.tile([P, TILES, PIXELS], F32, tag="att")
+            for j in range(TILES):
+                for t in range(TILES):
+                    nc.tensor.transpose(
+                        out=bank[:, j, P * t : P * (t + 1)],
+                        in_=att[i][:, t, P * j : P * (j + 1)],
+                        identity=ident[:],
+                    )
+            att_t[(hp, i)] = halves(work, [P, TILES, PIXELS], "att_t_%d" % i)
+            for j in range(TILES):
+                split(att_t[(hp, i)], (slice(None), j, band(j)), bank[:, j, band(j)])
 
         def weighted_sum(hp):
-            for i in range(PAIR):
-                part = [
-                    ps_att.tile([P, 2, BAND], F32, name="part_%d" % j, tag="att")
-                    for j in range(TILES)
-                ]
-                weights = att_t[hp][i]
-                for j in range(TILES):
+            overlap = BAND - BAND_STEP
+            res = [results.tile([P, 2, PIXELS], F32, name="res_%d" % i, tag="res") for i in range(PAIR)]
+            for j in range(TILES):
+                for i in range(PAIR):
+                    part = ps_att.tile([P, 2, BAND], F32, name="part", tag="att")
                     for c in range(2):
-                        if len(weights) == 1:
-                            terms = [(v_f32[hp][:, j, P * c : P * (c + 1)], weights[0][:, j, band(j)])]
-                        else:
-                            chan = slice(HEAD_DIM * i + P * c, HEAD_DIM * i + P * (c + 1))
-                            terms = [
-                                (v[hp][a][:, j, chan], weights[b][:, j, band(j)]) for a, b in PRODUCTS
-                            ]
-                        for n, (lhs, rhs) in enumerate(terms):
+                        chan = slice(HEAD_DIM * i + P * c, HEAD_DIM * i + P * (c + 1))
+                        for n, (a, b) in enumerate(PRODUCTS):
                             nc.tensor.matmul(
-                                out=part[j][:, c, :],
-                                lhsT=lhs,
-                                rhs=rhs,
+                                out=part[:, c, :],
+                                lhsT=v[hp][a][:, j, chan],
+                                rhs=att_t[(hp, i)][b][:, j, band(j)],
                                 start=(n == 0),
-                                stop=(n == len(terms) - 1),
+                                stop=(n == len(PRODUCTS) - 1),
                             )
-                res = results.tile([P, 2, PIXELS], F32, tag="res")
-                overlap = BAND - BAND_STEP
-                nc.vector.tensor_copy(out=res[:, :, 0:BAND], in_=part[0][:])
-                nc.scalar.copy(out=res[:, :, BAND:PIXELS], in_=part[1][:, :, overlap:BAND])
-                nc.vector.tensor_tensor(
-                    out=res[:, :, BAND_STEP:BAND],
-                    in0=res[:, :, BAND_STEP:BAND],
-                    in1=part[1][:, :, 0:overlap],
-                    op=ALU.add,
-                )
-                head = PAIR * hp + i
-                nc.sync.dma_start(out=out_rows[:, 2 * head : 2 * head + 2, :], in_=res[:])
+                    if j == 0:
+                        nc.vector.tensor_copy(out=res[i][:, :, 0:BAND], in_=part[:])
+                    else:
+                        nc.scalar.copy(out=res[i][:, :, BAND:PIXELS], in_=part[:, :, overlap:BAND])
+                        nc.vector.tensor_tensor(
+                            out=res[i][:, :, BAND_STEP:BAND],
+                            in0=res[i][:, :, BAND_STEP:BAND],
+                            in1=part[:, :, 0:overlap],
+                            op=ALU.add,
+                        )
+                        head = PAIR * hp + i
+                        nc.sync.dma_start(out=out_rows[:, 2 * head : 2 * head + 2, :], in_=res[i][:])
 
         for hp in range(pairs):
             q[hp] = halves(qkv, [P, 2 * PAIR, PIXELS], "q")
             k[hp] = halves(qkv, [P, 2 * PAIR, PIXELS], "k")
             v[hp] = halves(qkv, [P, TILES, PAIR_DIM], "v")
-            v_f32[hp] = None
-            if hp == pairs - 1:
-                v_f32[hp] = qkv.tile([P, TILES, HEAD_DIM], F32, name="v_f32", tag="v_f32", bufs=1)
-            project_channel_major(hp, 0, 0)
-            if hp == 1:
-                transpose_weights(0)
-            project_channel_major(hp, 0, 1)
-            project_channel_major(hp, 1, 0)
-            project_channel_major(hp, 1, 1)
-            project_pixel_major(hp, 0)
-            scores_and_weights(hp)
-            project_pixel_major(hp, 1)
+            for s in range(2):
+                for i in range(PAIR):
+                    project_channel_major(hp, s, i)
+            if hp > 0:
+                project_pixel_major(hp, [0])
+            for i in range(PAIR):
+                scores(hp, i)
+            if hp == 0:
+                project_pixel_major(hp, [0, 1])
+            else:
+                project_pixel_major(hp, [1])
             if hp + 2 < pairs:
                 load_pair(hp + 2)
             if hp > 0:
                 weighted_sum(hp - 1)
-                transpose_weights(hp)
+            for i in range(PAIR):
+                transpose_weights(hp, i)
         weighted_sum(pairs - 1)
 
 

@@ -32,6 +32,8 @@ BAND_STEP = PIXELS - BAND
 OUTSIDE = WINDOW - (REACH + 1) ** 2
 PAIR = 2
 PAIR_DIM = PAIR * HEAD_DIM
+PLANES_PER_TILE = 4
+PLANE_SLOTS = 2
 BIG = 1.0e30
 PRODUCTS = ((0, 0), (0, 1), (1, 0))
 
@@ -42,13 +44,20 @@ def band(t):
     return slice(BAND_STEP * t, BAND_STEP * t + BAND)
 
 
+def plane_rows(g):
+    return slice(PACK * (g % PLANES_PER_TILE), P)
+
+
+def plane_slot(g):
+    return g // PLANES_PER_TILE
+
+
 def tile_relation_w_kernel(tc, x, w_qkv_words, w_qkv_scales, out):
     nc = tc.nc
     pairs = HEADS // PAIR
 
     x_rows = x[0].rearrange("(g p t) h w -> p g t (h w)", g=PASSES, p=P, t=PACK)
     w_bytes = w_qkv_words.rearrange("g p n t -> p g (n t)")
-    w_scale_rows = w_qkv_scales.rearrange("g (q r) n -> q r g n", q=4)
     out_rows = out[0].rearrange("(a p) h w -> p a (h w)", p=P)
 
     with ExitStack() as stack:
@@ -63,11 +72,7 @@ def tile_relation_w_kernel(tc, x, w_qkv_words, w_qkv_scales, out):
             for b in range(2)
         ]
         w_planes = [
-            [
-                keep.tile([P, PASSES, PAIR_DIM], U8, name="w_planes_%d_%d" % (b, s), align_bytes=64)
-                for s in range(3)
-            ]
-            for b in range(2)
+            keep.tile([P, PLANE_SLOTS, D], U8, name="w_planes_%d" % s, align_bytes=64) for s in range(3)
         ]
         first_words = [
             [
@@ -77,7 +82,7 @@ def tile_relation_w_kernel(tc, x, w_qkv_words, w_qkv_scales, out):
             for s in range(2)
         ]
         x_words = keep.tile([P, PASSES, PIXELS], U32, align_bytes=64)
-        x_planes = keep.tile([P, PASSES, PIXELS], U8, align_bytes=64)
+        x_planes = keep.tile([P, PLANE_SLOTS, PIXELS], U8, align_bytes=64)
         ident = keep.tile([P, P], F32)
         cap = keep.tile([P, TILES, BAND], F32)
         masked = [
@@ -86,22 +91,24 @@ def tile_relation_w_kernel(tc, x, w_qkv_words, w_qkv_scales, out):
         att = [keep.tile([P, TILES, PIXELS], F32, name="att_%d" % i) for i in range(PAIR)]
         warm = keep.tile([P, 1], F32)
 
-        def clear_planes(engine, b, s):
-            engine.memset(w_planes[b][s][:].bitcast(I32), 0)
-
-        clear_planes(nc.vector, 0, 0)
-        clear_planes(nc.gpsimd, 0, 1)
-        clear_planes(nc.gpsimd, 0, 2)
+        nc.vector.memset(w_planes[0][:].bitcast(I32), 0)
+        for s in (1, 2):
+            nc.gpsimd.memset(w_planes[s][:].bitcast(I32), 0)
         nc.vector.memset(warm[:], 0.0)
         nc.scalar.activation(out=warm[:], in_=warm[:], func=FUNC.Exp)
 
-        def load_scales(hp, s):
-            first = s * D + hp * PAIR_DIM
-            for quad in range(4):
-                nc.sync.dma_start(
-                    out=w_planes[hp % 2][s][32 * quad : 32 * quad + PACK].bitcast(I32),
-                    in_=w_scale_rows[quad, :, :, first : first + PAIR_DIM].bitcast(I32),
-                )
+        def load_scales(s):
+            for slot in range(PLANE_SLOTS):
+                g_lo = slot * PLANES_PER_TILE
+                g_hi = min(g_lo + PLANES_PER_TILE, PASSES)
+                for quad in range(4):
+                    rows = slice(32 * quad, 32 * quad + PACK * (g_hi - g_lo))
+                    nc.sync.dma_start(
+                        out=w_planes[s][rows, slot, :].bitcast(I32),
+                        in_=w_qkv_scales[
+                            g_lo:g_hi, PACK * quad : PACK * (quad + 1), s * D : (s + 1) * D
+                        ].bitcast(I32),
+                    )
 
         def load_words(tile, first, passes=slice(0, PASSES)):
             width = tile.shape[2]
@@ -112,7 +119,6 @@ def tile_relation_w_kernel(tc, x, w_qkv_words, w_qkv_scales, out):
 
         def load_pair(hp):
             for s in range(3):
-                load_scales(hp, s)
                 load_words(w_words[hp % 2][s], s * D + hp * PAIR_DIM)
 
         mask_pool = stack.enter_context(tc.tile_pool(name="mask_pool", bufs=1))
@@ -120,14 +126,12 @@ def tile_relation_w_kernel(tc, x, w_qkv_words, w_qkv_scales, out):
             x_raw = setup.tile([P, PASSES, PACK, PIXELS], BF16)
             for g in range(0, PASSES, 2):
                 nc.sync.dma_start(out=x_raw[:, g : g + 2], in_=x_rows[:, g : g + 2])
-                if g == 2:
-                    load_scales(0, 0)
-            for i in range(PAIR):
-                load_words(first_words[0][i], HEAD_DIM * i)
-            load_scales(0, 1)
-            for i in range(PAIR):
-                load_words(first_words[1][i], D + HEAD_DIM * i)
-            load_scales(0, 2)
+            load_scales(0)
+            load_scales(1)
+            for s in range(2):
+                for i in range(PAIR):
+                    load_words(first_words[s][i], s * D + HEAD_DIM * i)
+            load_scales(2)
             half = PASSES // 2
             load_words(w_words[0][2], 2 * D, slice(0, half))
             load_words(w_words[0][2], 2 * D, slice(half, PASSES))
@@ -144,8 +148,6 @@ def tile_relation_w_kernel(tc, x, w_qkv_words, w_qkv_scales, out):
                     quantise_x(nc, x_grouped, x_words, x_planes, g - 1)
             quantise_x(nc, x_grouped, x_words, x_planes, PASSES - 1)
 
-        for s in range(3):
-            clear_planes(nc.vector, 1, s)
         for i in range(PAIR):
             nc.vector.memset(att[i][:], 0.0)
         load_pair(1)
@@ -175,14 +177,14 @@ def tile_relation_w_kernel(tc, x, w_qkv_words, w_qkv_scales, out):
             for c in range(2):
                 lo = P * c if hp == 0 else HEAD_DIM * i + P * c
                 words = first_words[s][i] if hp == 0 else w_words[hp % 2][s]
-                plane_lo = HEAD_DIM * i + P * c
+                plane_lo = hp * PAIR_DIM + HEAD_DIM * i + P * c
                 for g in range(PASSES):
                     nc.tensor.matmul_mx(
                         out=bank[:, c, :],
                         lhsT=words[:, g, lo : lo + P].bitcast(FP8X4),
-                        lhsT_scale=w_planes[hp % 2][s][:, g, plane_lo : plane_lo + P],
+                        lhsT_scale=w_planes[s][plane_rows(g), plane_slot(g), plane_lo : plane_lo + P],
                         rhs=x_words[:, g, :].bitcast(FP8X4),
-                        rhs_scale=x_planes[:, g, :],
+                        rhs_scale=x_planes[plane_rows(g), plane_slot(g), :],
                         start=(g == 0),
                         stop=(g == PASSES - 1),
                     )
@@ -201,9 +203,11 @@ def tile_relation_w_kernel(tc, x, w_qkv_words, w_qkv_scales, out):
                     nc.tensor.matmul_mx(
                         out=banks[t][:],
                         lhsT=x_words[:, g, pix].bitcast(FP8X4),
-                        lhsT_scale=x_planes[:, g, pix],
+                        lhsT_scale=x_planes[plane_rows(g), plane_slot(g), pix],
                         rhs=w_words[hp % 2][2][:, g, :].bitcast(FP8X4),
-                        rhs_scale=w_planes[hp % 2][2][:, g, :],
+                        rhs_scale=w_planes[2][
+                            plane_rows(g), plane_slot(g), hp * PAIR_DIM : (hp + 1) * PAIR_DIM
+                        ],
                         start=(g == 0),
                         stop=(g == PASSES - 1),
                     )
@@ -231,6 +235,9 @@ def tile_relation_w_kernel(tc, x, w_qkv_words, w_qkv_scales, out):
             nc.vector.tensor_reduce(
                 out=neg_max[:], in_=masked[i][:], axis=AXIS.X, op=ALU.max, negate=True
             )
+            return neg_max
+
+        def exponentials(i, neg_max):
             total = small.tile([P, TILES], F32, tag="total")
             exps = work.tile([P, TILES, BAND + OUTSIDE], F32, tag="exps")
             for t in range(TILES):
@@ -242,6 +249,9 @@ def tile_relation_w_kernel(tc, x, w_qkv_words, w_qkv_scales, out):
                     scale=1.0,
                     accum_out=total[:, t : t + 1],
                 )
+            return exps, total
+
+        def normalise(i, exps, total):
             inv_total = small.tile([P, TILES], F32, tag="inv_total")
             nc.vector.reciprocal(out=inv_total[:], in_=total[:])
             for t in range(TILES):
@@ -304,8 +314,10 @@ def tile_relation_w_kernel(tc, x, w_qkv_words, w_qkv_scales, out):
                     project_channel_major(hp, s, i)
             if hp > 0:
                 project_pixel_major(hp, [0])
+            neg_max = [scores(hp, i) for i in range(PAIR)]
+            exps = [exponentials(i, neg_max[i]) for i in range(PAIR)]
             for i in range(PAIR):
-                scores(hp, i)
+                normalise(i, exps[i][0], exps[i][1])
             if hp == 0:
                 project_pixel_major(hp, [0, 1])
             else:
@@ -322,7 +334,7 @@ def tile_relation_w_kernel(tc, x, w_qkv_words, w_qkv_scales, out):
 def quantise_x(nc, x_grouped, x_words, x_planes, g):
     nc.vector.quantize_mx(
         out=x_words[:, g, :].bitcast(FP8X4),
-        scales=x_planes[:, g, :],
+        scales=x_planes[plane_rows(g), plane_slot(g), :],
         in_=x_grouped[:, g].rearrange("p n t -> p (n t)"),
     )
 

@@ -72,14 +72,15 @@ def tile_relation_w_kernel(tc, x, w_qkv_words, w_qkv_scales, out):
             for b in range(2)
         ]
         w_planes = [
-            keep.tile([P, PLANE_SLOTS, D], U8, name="w_planes_%d" % s, align_bytes=64) for s in range(3)
+            [
+                keep.tile([P, PLANE_SLOTS, 2 * PAIR_DIM], U8, name="w_planes_%d_%d" % (s, b), align_bytes=64)
+                for b in range(pairs // 2)
+            ]
+            for s in range(3)
         ]
         first_words = [
-            [
-                keep.tile([P, PASSES, HEAD_DIM], U32, name="first_words_%d_%d" % (s, i), align_bytes=64)
-                for i in range(PAIR)
-            ]
-            for s in range(2)
+            keep.tile([P, PASSES, HEAD_DIM], U32, name="first_words_%d" % i, align_bytes=64)
+            for i in range(PAIR)
         ]
         x_words = keep.tile([P, PASSES, PIXELS], U32, align_bytes=64)
         x_planes = keep.tile([P, PLANE_SLOTS, PIXELS], U8, align_bytes=64)
@@ -91,50 +92,52 @@ def tile_relation_w_kernel(tc, x, w_qkv_words, w_qkv_scales, out):
         att = [keep.tile([P, TILES, PIXELS], F32, name="att_%d" % i) for i in range(PAIR)]
         warm = keep.tile([P, 1], F32)
 
-        nc.vector.memset(w_planes[0][:].bitcast(I32), 0)
+        nc.vector.memset(w_planes[0][0][:].bitcast(I32), 0)
         for s in (1, 2):
-            nc.gpsimd.memset(w_planes[s][:].bitcast(I32), 0)
+            nc.gpsimd.memset(w_planes[s][0][:].bitcast(I32), 0)
         nc.vector.memset(warm[:], 0.0)
         nc.scalar.activation(out=warm[:], in_=warm[:], func=FUNC.Exp)
 
-        def load_scales(s):
-            for slot in range(PLANE_SLOTS):
+        def load_scales(s, b, first, last):
+            lo = s * D + b * 2 * PAIR_DIM
+            for n in range(first, last):
+                slot, quad = divmod(n, 4)
                 g_lo = slot * PLANES_PER_TILE
                 g_hi = min(g_lo + PLANES_PER_TILE, PASSES)
-                for quad in range(4):
-                    rows = slice(32 * quad, 32 * quad + PACK * (g_hi - g_lo))
-                    nc.sync.dma_start(
-                        out=w_planes[s][rows, slot, :].bitcast(I32),
-                        in_=w_qkv_scales[
-                            g_lo:g_hi, PACK * quad : PACK * (quad + 1), s * D : (s + 1) * D
-                        ].bitcast(I32),
-                    )
+                rows = slice(32 * quad, 32 * quad + PACK * (g_hi - g_lo))
+                nc.sync.dma_start(
+                    out=w_planes[s][b][rows, slot, :].bitcast(I32),
+                    in_=w_qkv_scales[
+                        g_lo:g_hi, PACK * quad : PACK * (quad + 1), lo : lo + 2 * PAIR_DIM
+                    ].bitcast(I32),
+                )
 
-        def load_words(tile, first, passes=slice(0, PASSES)):
+        def load_words(tile, first):
             width = tile.shape[2]
             nc.sync.dma_start(
-                out=tile[:, passes, :].bitcast(I32),
-                in_=w_bytes[:, passes, PACK * first : PACK * (first + width)].bitcast(I32),
+                out=tile[:].bitcast(I32), in_=w_bytes[:, :, PACK * first : PACK * (first + width)].bitcast(I32)
             )
 
-        def load_pair(hp):
-            for s in range(3):
-                load_words(w_words[hp % 2][s], s * D + hp * PAIR_DIM)
+        def load_kind(hp, s):
+            load_words(w_words[hp % 2][s], s * D + hp * PAIR_DIM)
 
         mask_pool = stack.enter_context(tc.tile_pool(name="mask_pool", bufs=1))
         with tc.tile_pool(name="setup", bufs=1) as setup:
+            load_scales(0, 0, 0, 4)
             x_raw = setup.tile([P, PASSES, PACK, PIXELS], BF16)
             for g in range(0, PASSES, 2):
                 nc.sync.dma_start(out=x_raw[:, g : g + 2], in_=x_rows[:, g : g + 2])
-            load_scales(0)
-            load_scales(1)
-            for s in range(2):
-                for i in range(PAIR):
-                    load_words(first_words[s][i], s * D + HEAD_DIM * i)
-            load_scales(2)
-            half = PASSES // 2
-            load_words(w_words[0][2], 2 * D, slice(0, half))
-            load_words(w_words[0][2], 2 * D, slice(half, PASSES))
+            load_scales(0, 0, 4, 8)
+            for i in range(PAIR):
+                load_words(first_words[i], HEAD_DIM * i)
+            load_scales(1, 0, 0, 4)
+            load_kind(0, 1)
+            load_scales(1, 0, 4, 8)
+            load_scales(2, 0, 0, 2)
+            load_kind(0, 2)
+            load_scales(2, 0, 2, 8)
+            for s in range(3):
+                load_kind(1, s)
 
             build_mask(nc, mask_pool, cap, masked)
             make_identity(nc, ident[:])
@@ -148,9 +151,10 @@ def tile_relation_w_kernel(tc, x, w_qkv_words, w_qkv_scales, out):
                     quantise_x(nc, x_grouped, x_words, x_planes, g - 1)
             quantise_x(nc, x_grouped, x_words, x_planes, PASSES - 1)
 
+        for s in range(3):
+            nc.vector.memset(w_planes[s][1][:].bitcast(I32), 0)
         for i in range(PAIR):
             nc.vector.memset(att[i][:], 0.0)
-        load_pair(1)
 
         qkv = stack.enter_context(tc.tile_pool(name="qkv", bufs=2))
         work = stack.enter_context(tc.tile_pool(name="work", bufs=2))
@@ -175,14 +179,16 @@ def tile_relation_w_kernel(tc, x, w_qkv_words, w_qkv_scales, out):
         def project_channel_major(hp, s, i):
             bank = ps_proj.tile([P, 2, PIXELS], F32, tag="proj")
             for c in range(2):
-                lo = P * c if hp == 0 else HEAD_DIM * i + P * c
-                words = first_words[s][i] if hp == 0 else w_words[hp % 2][s]
-                plane_lo = hp * PAIR_DIM + HEAD_DIM * i + P * c
+                if hp == 0 and s == 0:
+                    words, lo = first_words[i], P * c
+                else:
+                    words, lo = w_words[hp % 2][s], HEAD_DIM * i + P * c
+                plane_lo = (hp % 2) * PAIR_DIM + HEAD_DIM * i + P * c
                 for g in range(PASSES):
                     nc.tensor.matmul_mx(
                         out=bank[:, c, :],
                         lhsT=words[:, g, lo : lo + P].bitcast(FP8X4),
-                        lhsT_scale=w_planes[s][plane_rows(g), plane_slot(g), plane_lo : plane_lo + P],
+                        lhsT_scale=w_planes[s][hp // 2][plane_rows(g), plane_slot(g), plane_lo : plane_lo + P],
                         rhs=x_words[:, g, :].bitcast(FP8X4),
                         rhs_scale=x_planes[plane_rows(g), plane_slot(g), :],
                         start=(g == 0),
@@ -194,6 +200,7 @@ def tile_relation_w_kernel(tc, x, w_qkv_words, w_qkv_scales, out):
                 split((q, k)[s][hp], (slice(None), slice(2 * i, 2 * i + 2), slice(None)), bank[:])
 
         def project_pixel_major(hp, tiles):
+            plane_cols = slice((hp % 2) * PAIR_DIM, (hp % 2 + 1) * PAIR_DIM)
             banks = {}
             for t in tiles:
                 banks[t] = ps_proj.tile([P, PAIR_DIM], F32, name="v_bank_%d" % t, tag="proj")
@@ -205,9 +212,7 @@ def tile_relation_w_kernel(tc, x, w_qkv_words, w_qkv_scales, out):
                         lhsT=x_words[:, g, pix].bitcast(FP8X4),
                         lhsT_scale=x_planes[plane_rows(g), plane_slot(g), pix],
                         rhs=w_words[hp % 2][2][:, g, :].bitcast(FP8X4),
-                        rhs_scale=w_planes[2][
-                            plane_rows(g), plane_slot(g), hp * PAIR_DIM : (hp + 1) * PAIR_DIM
-                        ],
+                        rhs_scale=w_planes[2][hp // 2][plane_rows(g), plane_slot(g), plane_cols],
                         start=(g == 0),
                         stop=(g == PASSES - 1),
                     )
@@ -322,8 +327,19 @@ def tile_relation_w_kernel(tc, x, w_qkv_words, w_qkv_scales, out):
                 project_pixel_major(hp, [0, 1])
             else:
                 project_pixel_major(hp, [1])
-            if hp + 2 < pairs:
-                load_pair(hp + 2)
+            if hp == 0:
+                load_scales(0, 1, 0, 6)
+                load_kind(2, 0)
+                load_scales(0, 1, 6, 8)
+                load_scales(1, 1, 0, 4)
+                load_kind(2, 1)
+                load_scales(1, 1, 4, 8)
+                load_scales(2, 1, 0, 2)
+                load_kind(2, 2)
+                load_scales(2, 1, 2, 8)
+            elif hp == 1:
+                for s in range(3):
+                    load_kind(3, s)
             if hp > 0:
                 weighted_sum(hp - 1)
             for i in range(PAIR):

@@ -34,6 +34,7 @@ PAIR = 2
 PAIR_DIM = PAIR * HEAD_DIM
 PLANES_PER_TILE = 4
 PLANE_SLOTS = 2
+WARM_PASSES = 10
 BIG = 1.0e30
 PRODUCTS = ((0, 0), (0, 1), (1, 0))
 
@@ -83,7 +84,7 @@ def tile_relation_w_kernel(tc, x, w_qkv_words, w_qkv_scales, out):
             for i in range(PAIR)
         ]
         x_words = keep.tile([P, PASSES, PIXELS], U32, align_bytes=64)
-        x_planes = keep.tile([P, PLANE_SLOTS, PIXELS], U8, align_bytes=64)
+        x_planes = keep.tile([P, PASSES, PIXELS], U8, align_bytes=64)
         ident = keep.tile([P, P], F32)
         cap = keep.tile([P, TILES, BAND], F32)
         masked = [
@@ -121,12 +122,29 @@ def tile_relation_w_kernel(tc, x, w_qkv_words, w_qkv_scales, out):
         def load_kind(hp, s):
             load_words(w_words[hp % 2][s], s * D + hp * PAIR_DIM)
 
+        ps_proj = stack.enter_context(tc.psum_pool(name="ps_proj", bufs=3))
+        ps_att = stack.enter_context(tc.psum_pool(name="ps_att", bufs=5))
+
+        def warm_up():
+            bank = ps_att.tile([P, PIXELS], F32, name="warm_bank", tag="att")
+            for n in range(WARM_PASSES):
+                nc.tensor.matmul_mx(
+                    out=bank[:],
+                    lhsT=x_words[:, 0, 0:P].bitcast(FP8X4),
+                    lhsT_scale=x_planes[:, 0, 0:P],
+                    rhs=x_words[:, 0, :].bitcast(FP8X4),
+                    rhs_scale=x_planes[:, 0, :],
+                    start=(n == 0),
+                    stop=(n == WARM_PASSES - 1),
+                )
+
         mask_pool = stack.enter_context(tc.tile_pool(name="mask_pool", bufs=1))
         with tc.tile_pool(name="setup", bufs=1) as setup:
-            load_scales(0, 0, 0, 4)
             x_raw = setup.tile([P, PASSES, PACK, PIXELS], BF16)
             for g in range(0, PASSES, 2):
                 nc.sync.dma_start(out=x_raw[:, g : g + 2], in_=x_rows[:, g : g + 2])
+                if g == 0:
+                    load_scales(0, 0, 0, 4)
             load_scales(0, 0, 4, 8)
             for i in range(PAIR):
                 load_words(first_words[i], HEAD_DIM * i)
@@ -149,6 +167,8 @@ def tile_relation_w_kernel(tc, x, w_qkv_words, w_qkv_scales, out):
                 nc.vector.tensor_copy(out=x_grouped[:, g, P:PIXELS, :], in_=rows[:, P:PIXELS, :])
                 if g > 0:
                     quantise_x(nc, x_grouped, x_words, x_planes, g - 1)
+                if g == 1:
+                    warm_up()
             quantise_x(nc, x_grouped, x_words, x_planes, PASSES - 1)
 
         for s in range(3):
@@ -160,8 +180,6 @@ def tile_relation_w_kernel(tc, x, w_qkv_words, w_qkv_scales, out):
         work = stack.enter_context(tc.tile_pool(name="work", bufs=2))
         small = stack.enter_context(tc.tile_pool(name="small", bufs=4))
         results = stack.enter_context(tc.tile_pool(name="results", bufs=HEADS))
-        ps_proj = stack.enter_context(tc.psum_pool(name="ps_proj", bufs=3))
-        ps_att = stack.enter_context(tc.psum_pool(name="ps_att", bufs=5))
 
         q, k, v, att_t = {}, {}, {}, {}
         whole = [
@@ -190,7 +208,7 @@ def tile_relation_w_kernel(tc, x, w_qkv_words, w_qkv_scales, out):
                         lhsT=words[:, g, lo : lo + P].bitcast(FP8X4),
                         lhsT_scale=w_planes[s][hp // 2][plane_rows(g), plane_slot(g), plane_lo : plane_lo + P],
                         rhs=x_words[:, g, :].bitcast(FP8X4),
-                        rhs_scale=x_planes[plane_rows(g), plane_slot(g), :],
+                        rhs_scale=x_planes[:, g, :],
                         start=(g == 0),
                         stop=(g == PASSES - 1),
                     )
@@ -210,7 +228,7 @@ def tile_relation_w_kernel(tc, x, w_qkv_words, w_qkv_scales, out):
                     nc.tensor.matmul_mx(
                         out=banks[t][:],
                         lhsT=x_words[:, g, pix].bitcast(FP8X4),
-                        lhsT_scale=x_planes[plane_rows(g), plane_slot(g), pix],
+                        lhsT_scale=x_planes[:, g, pix],
                         rhs=w_words[hp % 2][2][:, g, :].bitcast(FP8X4),
                         rhs_scale=w_planes[2][hp // 2][plane_rows(g), plane_slot(g), plane_cols],
                         start=(g == 0),
@@ -350,7 +368,7 @@ def tile_relation_w_kernel(tc, x, w_qkv_words, w_qkv_scales, out):
 def quantise_x(nc, x_grouped, x_words, x_planes, g):
     nc.vector.quantize_mx(
         out=x_words[:, g, :].bitcast(FP8X4),
-        scales=x_planes[plane_rows(g), plane_slot(g), :],
+        scales=x_planes[:, g, :],
         in_=x_grouped[:, g].rearrange("p n t -> p (n t)"),
     )
 

@@ -28,21 +28,23 @@ TILES = PIXELS // P
 TILE_ROWS = P // SIDE
 BAND_ROWS = TILE_ROWS + REACH
 BAND = BAND_ROWS * SIDE
-BAND_STEP = PIXELS - BAND
+EDGE = REACH * SIDE
+KEY_ROWS = (((8, 2), (0, 8)), ((6, 2), (10, 6), (8, 2)))
 OUTSIDE = WINDOW - (REACH + 1) ** 2
 PAIR = 2
 PAIR_DIM = PAIR * HEAD_DIM
 PLANES_PER_TILE = 4
 PLANE_SLOTS = 2
-WARM_PASSES = 10
+WARM_PASSES = 16
+FIRST_PIECES = (slice(0, PASSES // 2), slice(PASSES // 2, PASSES))
 BIG = 1.0e30
-PRODUCTS = ((0, 0), (0, 1), (1, 0))
+PRODUCTS = ((0, 0), (1, 0), (0, 1))
 
 FLOPS = 2 * 3 * D * C_IN * PIXELS + 2 * 2 * D * WINDOW * PIXELS
 
 
 def band(t):
-    return slice(BAND_STEP * t, BAND_STEP * t + BAND)
+    return slice(P * t, P * t + BAND)
 
 
 def plane_rows(g):
@@ -79,10 +81,6 @@ def tile_relation_w_kernel(tc, x, w_qkv_words, w_qkv_scales, out):
             ]
             for s in range(3)
         ]
-        first_words = [
-            keep.tile([P, PASSES, HEAD_DIM], U32, name="first_words_%d" % i, align_bytes=64)
-            for i in range(PAIR)
-        ]
         x_words = keep.tile([P, PASSES, PIXELS], U32, align_bytes=64)
         x_planes = keep.tile([P, PASSES, PIXELS], U8, align_bytes=64)
         ident = keep.tile([P, P], F32)
@@ -90,14 +88,17 @@ def tile_relation_w_kernel(tc, x, w_qkv_words, w_qkv_scales, out):
         masked = [
             keep.tile([P, TILES, BAND + OUTSIDE], F32, name="masked_%d" % i) for i in range(PAIR)
         ]
-        att = [keep.tile([P, TILES, PIXELS], F32, name="att_%d" % i) for i in range(PAIR)]
+        att = [keep.tile([P, TILES, BAND], F32, name="att_%d" % i, align_bytes=64) for i in range(PAIR)]
         warm = keep.tile([P, 1], F32)
 
         nc.vector.memset(w_planes[0][0][:].bitcast(I32), 0)
-        for s in (1, 2):
-            nc.gpsimd.memset(w_planes[s][0][:].bitcast(I32), 0)
         nc.vector.memset(warm[:], 0.0)
         nc.scalar.activation(out=warm[:], in_=warm[:], func=FUNC.Exp)
+        mask_pool = stack.enter_context(tc.tile_pool(name="mask_pool", bufs=1))
+        build_mask(nc, mask_pool, cap, masked)
+        for s in (1, 2):
+            nc.gpsimd.memset(w_planes[s][0][:].bitcast(I32), 0)
+        make_identity(nc, ident[:])
 
         def load_scales(s, b, first, last):
             lo = s * D + b * 2 * PAIR_DIM
@@ -113,14 +114,12 @@ def tile_relation_w_kernel(tc, x, w_qkv_words, w_qkv_scales, out):
                     ].bitcast(I32),
                 )
 
-        def load_words(tile, first):
-            width = tile.shape[2]
+        def load_kind(hp, s, passes=slice(0, PASSES)):
+            first = PACK * (s * D + hp * PAIR_DIM)
             nc.sync.dma_start(
-                out=tile[:].bitcast(I32), in_=w_bytes[:, :, PACK * first : PACK * (first + width)].bitcast(I32)
+                out=w_words[hp % 2][s][:, passes, :].bitcast(I32),
+                in_=w_bytes[:, passes, first : first + PACK * PAIR_DIM].bitcast(I32),
             )
-
-        def load_kind(hp, s):
-            load_words(w_words[hp % 2][s], s * D + hp * PAIR_DIM)
 
         ps_proj = stack.enter_context(tc.psum_pool(name="ps_proj", bufs=3))
         ps_att = stack.enter_context(tc.psum_pool(name="ps_att", bufs=5))
@@ -138,7 +137,6 @@ def tile_relation_w_kernel(tc, x, w_qkv_words, w_qkv_scales, out):
                     stop=(n == WARM_PASSES - 1),
                 )
 
-        mask_pool = stack.enter_context(tc.tile_pool(name="mask_pool", bufs=1))
         with tc.tile_pool(name="setup", bufs=1) as setup:
             x_raw = setup.tile([P, PASSES, PACK, PIXELS], BF16)
             for g in range(0, PASSES, 2):
@@ -146,25 +144,24 @@ def tile_relation_w_kernel(tc, x, w_qkv_words, w_qkv_scales, out):
                 if g == 0:
                     load_scales(0, 0, 0, 4)
             load_scales(0, 0, 4, 8)
-            for i in range(PAIR):
-                load_words(first_words[i], HEAD_DIM * i)
-            load_scales(1, 0, 0, 4)
-            load_kind(0, 1)
-            load_scales(1, 0, 4, 8)
+            for passes in FIRST_PIECES:
+                load_kind(0, 0, passes)
+            load_scales(1, 0, 0, 5)
+            for passes in FIRST_PIECES:
+                load_kind(0, 1, passes)
+            load_scales(1, 0, 5, 8)
             load_scales(2, 0, 0, 2)
             load_kind(0, 2)
             load_scales(2, 0, 2, 8)
             for s in range(3):
                 load_kind(1, s)
 
-            build_mask(nc, mask_pool, cap, masked)
-            make_identity(nc, ident[:])
-
             x_grouped = setup.tile([P, PASSES, PIXELS, PACK], BF16, align_bytes=64)
             for g in range(PASSES):
                 rows = x_raw[:, g].rearrange("p t n -> p n t")
                 nc.scalar.copy(out=x_grouped[:, g, 0:P, :], in_=rows[:, 0:P, :])
-                nc.vector.tensor_copy(out=x_grouped[:, g, P:PIXELS, :], in_=rows[:, P:PIXELS, :])
+                nc.vector.tensor_copy(out=x_grouped[:, g, P : PIXELS - EDGE, :], in_=rows[:, P + EDGE : PIXELS, :])
+                nc.scalar.copy(out=x_grouped[:, g, PIXELS - EDGE : PIXELS, :], in_=rows[:, P : P + EDGE, :])
                 if g > 0:
                     quantise_x(nc, x_grouped, x_words, x_planes, g - 1)
                 if g == 1:
@@ -173,8 +170,6 @@ def tile_relation_w_kernel(tc, x, w_qkv_words, w_qkv_scales, out):
 
         for s in range(3):
             nc.vector.memset(w_planes[s][1][:].bitcast(I32), 0)
-        for i in range(PAIR):
-            nc.vector.memset(att[i][:], 0.0)
 
         qkv = stack.enter_context(tc.tile_pool(name="qkv", bufs=2))
         work = stack.enter_context(tc.tile_pool(name="work", bufs=2))
@@ -183,24 +178,48 @@ def tile_relation_w_kernel(tc, x, w_qkv_words, w_qkv_scales, out):
 
         q, k, v, att_t = {}, {}, {}, {}
         whole = [
-            qkv.tile([P, 2, PIXELS], F32, name="whole_%d" % s, tag="whole_%d" % s, bufs=1) for s in range(2)
+            qkv.tile([P, 2, PIXELS + EDGE * s], F32, name="whole_%d" % s, tag="whole_%d" % s, bufs=1)
+            for s in range(2)
         ]
 
-        def halves(pool, shape, name):
-            return [pool.tile(shape, BF16, name=name + h, tag=name + h) for h in ("_hi", "_lo")]
+        def split(*pieces):
+            pieces = list(zip(pieces[0::2], pieces[1::2]))
+            for halves, values in pieces:
+                nc.scalar.copy(out=halves[0], in_=values)
+            for halves, values in pieces:
+                nc.vector.tensor_tensor(out=halves[1], in0=values, in1=halves[0], op=ALU.subtract)
 
-        def split(dest, where, bank):
-            hi, lo = dest
-            nc.scalar.copy(out=hi[where], in_=bank)
-            nc.vector.tensor_tensor(out=lo[where], in0=bank, in1=hi[where], op=ALU.subtract)
+        def project_first(s):
+            banks = [ps_att.tile([P, PIXELS], F32, name="bank_%d" % c, tag="att") for c in range(2 * PAIR)]
+            for passes in FIRST_PIECES:
+                for c in range(2 * PAIR):
+                    for g in range(passes.start, passes.stop):
+                        nc.tensor.matmul_mx(
+                            out=banks[c][:],
+                            lhsT=w_words[0][s][:, g, P * c : P * (c + 1)].bitcast(FP8X4),
+                            lhsT_scale=w_planes[s][0][plane_rows(g), plane_slot(g), P * c : P * (c + 1)],
+                            rhs=x_words[:, g, :].bitcast(FP8X4),
+                            rhs_scale=x_planes[:, g, :],
+                            start=(g == 0),
+                            stop=(g == PASSES - 1),
+                        )
+            for c in range(2 * PAIR):
+                if c < 2:
+                    nc.scalar.copy(out=whole[s][:, c, EDGE * s : EDGE * s + PIXELS], in_=banks[c][:])
+                    if s == 1:
+                        nc.scalar.copy(out=whole[1][:, c, 0:EDGE], in_=banks[c][:, PIXELS - EDGE : PIXELS])
+                elif s == 0:
+                    split([q[0][:, a, c, :] for a in range(2)], banks[c][:])
+                else:
+                    split(
+                        [k[0][:, a, c, EDGE : EDGE + PIXELS] for a in range(2)], banks[c][:],
+                        [k[0][:, a, c, 0:EDGE] for a in range(2)], banks[c][:, PIXELS - EDGE : PIXELS],
+                    )
 
         def project_channel_major(hp, s, i):
             bank = ps_proj.tile([P, 2, PIXELS], F32, tag="proj")
             for c in range(2):
-                if hp == 0 and s == 0:
-                    words, lo = first_words[i], P * c
-                else:
-                    words, lo = w_words[hp % 2][s], HEAD_DIM * i + P * c
+                words, lo = w_words[hp % 2][s], HEAD_DIM * i + P * c
                 plane_lo = (hp % 2) * PAIR_DIM + HEAD_DIM * i + P * c
                 for g in range(PASSES):
                     nc.tensor.matmul_mx(
@@ -212,30 +231,34 @@ def tile_relation_w_kernel(tc, x, w_qkv_words, w_qkv_scales, out):
                         start=(g == 0),
                         stop=(g == PASSES - 1),
                     )
+            chans = slice(2 * i, 2 * i + 2)
             if hp == 0 and i == 0:
-                nc.scalar.copy(out=whole[s][:], in_=bank[:])
+                nc.scalar.copy(out=whole[s][:, :, EDGE * s : EDGE * s + PIXELS], in_=bank[:])
+                if s == 1:
+                    nc.scalar.copy(out=whole[1][:, :, 0:EDGE], in_=bank[:, :, PIXELS - EDGE : PIXELS])
+            elif s == 0:
+                split([q[hp][:, a, chans, :] for a in range(2)], bank[:])
             else:
-                split((q, k)[s][hp], (slice(None), slice(2 * i, 2 * i + 2), slice(None)), bank[:])
+                split(
+                    [k[hp][:, a, chans, EDGE : EDGE + PIXELS] for a in range(2)], bank[:],
+                    [k[hp][:, a, chans, 0:EDGE] for a in range(2)], bank[:, :, PIXELS - EDGE : PIXELS],
+                )
 
-        def project_pixel_major(hp, tiles):
-            plane_cols = slice((hp % 2) * PAIR_DIM, (hp % 2 + 1) * PAIR_DIM)
-            banks = {}
-            for t in tiles:
-                banks[t] = ps_proj.tile([P, PAIR_DIM], F32, name="v_bank_%d" % t, tag="proj")
+        def project_pixel_major(hp, t, lo=0, hi=PAIR_DIM):
+            plane_cols = slice((hp % 2) * PAIR_DIM + lo, (hp % 2) * PAIR_DIM + hi)
+            bank = ps_proj.tile([P, hi - lo], F32, name="v_bank", tag="proj")
+            pix = slice(P * t, P * (t + 1))
             for g in range(PASSES):
-                for t in tiles:
-                    pix = slice(P * t, P * (t + 1))
-                    nc.tensor.matmul_mx(
-                        out=banks[t][:],
-                        lhsT=x_words[:, g, pix].bitcast(FP8X4),
-                        lhsT_scale=x_planes[:, g, pix],
-                        rhs=w_words[hp % 2][2][:, g, :].bitcast(FP8X4),
-                        rhs_scale=w_planes[2][hp // 2][plane_rows(g), plane_slot(g), plane_cols],
-                        start=(g == 0),
-                        stop=(g == PASSES - 1),
-                    )
-            for t in tiles:
-                split(v[hp], (slice(None), t, slice(None)), banks[t][:])
+                nc.tensor.matmul_mx(
+                    out=bank[:],
+                    lhsT=x_words[:, g, pix].bitcast(FP8X4),
+                    lhsT_scale=x_planes[:, g, pix],
+                    rhs=w_words[hp % 2][2][:, g, lo:hi].bitcast(FP8X4),
+                    rhs_scale=w_planes[2][hp // 2][plane_rows(g), plane_slot(g), plane_cols],
+                    start=(g == 0),
+                    stop=(g == PASSES - 1),
+                )
+            split([v[hp][:, a, t, lo:hi] for a in range(2)], bank[:])
 
         def scores(hp, i):
             score = ps_att.tile([P, TILES, BAND], F32, tag="att")
@@ -245,7 +268,7 @@ def tile_relation_w_kernel(tc, x, w_qkv_words, w_qkv_scales, out):
                     terms = [(whole[0][:, c, pix], whole[1][:, c, band(t)]) for c in range(2)]
                 else:
                     terms = [
-                        (q[hp][a][:, 2 * i + c, pix], k[hp][b][:, 2 * i + c, band(t)])
+                        (q[hp][:, a, 2 * i + c, pix], k[hp][:, b, 2 * i + c, band(t)])
                         for a, b in PRODUCTS
                         for c in range(2)
                     ]
@@ -279,28 +302,31 @@ def tile_relation_w_kernel(tc, x, w_qkv_words, w_qkv_scales, out):
             nc.vector.reciprocal(out=inv_total[:], in_=total[:])
             for t in range(TILES):
                 nc.vector.tensor_scalar(
-                    out=att[i][:, t, band(t)],
+                    out=att[i][:, t, :],
                     in0=exps[:, t, 0:BAND],
                     scalar1=inv_total[:, t : t + 1],
                     scalar2=None,
                     op0=ALU.mult,
                 )
 
-        def transpose_weights(hp, i):
-            bank = ps_att.tile([P, TILES, PIXELS], F32, tag="att")
-            for j in range(TILES):
-                for t in range(TILES):
-                    nc.tensor.transpose(
-                        out=bank[:, j, P * t : P * (t + 1)],
-                        in_=att[i][:, t, P * j : P * (j + 1)],
-                        identity=ident[:],
-                    )
-            att_t[(hp, i)] = halves(work, [P, TILES, PIXELS], "att_t_%d" % i)
-            for j in range(TILES):
-                split(att_t[(hp, i)], (slice(None), j, band(j)), bank[:, j, band(j)])
+        edges = {}
+
+        def turn_edges(i):
+            edges[i] = work.tile([P, TILES, EDGE], F32, name="edge_%d" % i, tag="edge_%d" % i, align_bytes=64)
+            for t in range(TILES):
+                nc.vector.transpose(out=edges[i][:, 1 - t, :], in_=att[i][:, t, 0:EDGE])
+
+        def turn_tiles(hp, i):
+            bank = ps_att.tile([P, TILES, P], F32, name="own", tag="att")
+            for t in range(TILES):
+                nc.tensor.transpose(out=bank[:, t, :], in_=att[i][:, t, EDGE:BAND], identity=ident[:])
+            att_t[(hp, i)] = work.tile([P, 2, TILES, BAND], BF16, name="att_t_%d" % i, tag="att_t_%d" % i)
+            split(
+                [att_t[(hp, i)][:, a, :, EDGE:BAND] for a in range(2)], bank[:],
+                [att_t[(hp, i)][:, a, :, 0:EDGE] for a in range(2)], edges[i][:],
+            )
 
         def weighted_sum(hp):
-            overlap = BAND - BAND_STEP
             res = [results.tile([P, 2, PIXELS], F32, name="res_%d" % i, tag="res") for i in range(PAIR)]
             for j in range(TILES):
                 for i in range(PAIR):
@@ -310,41 +336,33 @@ def tile_relation_w_kernel(tc, x, w_qkv_words, w_qkv_scales, out):
                         for n, (a, b) in enumerate(PRODUCTS):
                             nc.tensor.matmul(
                                 out=part[:, c, :],
-                                lhsT=v[hp][a][:, j, chan],
-                                rhs=att_t[(hp, i)][b][:, j, band(j)],
+                                lhsT=v[hp][:, a, j, chan],
+                                rhs=att_t[(hp, i)][:, b, j, :],
                                 start=(n == 0),
                                 stop=(n == len(PRODUCTS) - 1),
                             )
                     if j == 0:
-                        nc.vector.tensor_copy(out=res[i][:, :, 0:BAND], in_=part[:])
+                        nc.scalar.copy(out=res[i][:, :, P : P + EDGE], in_=part[:, :, 0:EDGE])
+                        nc.vector.tensor_copy(out=res[i][:, :, 0:P], in_=part[:, :, EDGE:BAND])
                     else:
-                        nc.scalar.copy(out=res[i][:, :, BAND:PIXELS], in_=part[:, :, overlap:BAND])
-                        nc.vector.tensor_tensor(
-                            out=res[i][:, :, BAND_STEP:BAND],
-                            in0=res[i][:, :, BAND_STEP:BAND],
-                            in1=part[:, :, 0:overlap],
-                            op=ALU.add,
-                        )
+                        nc.scalar.copy(out=res[i][:, :, P + EDGE : PIXELS], in_=part[:, :, EDGE:P])
+                        both = res[i][:, :, P - EDGE : P + EDGE].rearrange("p c (s w) -> p c s w", w=EDGE)
+                        ends = part[:].rearrange("p c (s w) -> p c s w", w=EDGE)[:, :, 0 : BAND_ROWS // REACH : P // EDGE, :]
+                        nc.vector.tensor_tensor(out=both, in0=both, in1=ends, op=ALU.add)
                         head = PAIR * hp + i
                         nc.sync.dma_start(out=out_rows[:, 2 * head : 2 * head + 2, :], in_=res[i][:])
 
-        for hp in range(pairs):
-            q[hp] = halves(qkv, [P, 2 * PAIR, PIXELS], "q")
-            k[hp] = halves(qkv, [P, 2 * PAIR, PIXELS], "k")
-            v[hp] = halves(qkv, [P, TILES, PAIR_DIM], "v")
-            for s in range(2):
-                for i in range(PAIR):
-                    project_channel_major(hp, s, i)
-            if hp > 0:
-                project_pixel_major(hp, [0])
+        def attend(hp):
             neg_max = [scores(hp, i) for i in range(PAIR)]
-            exps = [exponentials(i, neg_max[i]) for i in range(PAIR)]
+            return [exponentials(i, neg_max[i]) for i in range(PAIR)]
+
+        def finish(exps):
             for i in range(PAIR):
                 normalise(i, exps[i][0], exps[i][1])
-            if hp == 0:
-                project_pixel_major(hp, [0, 1])
-            else:
-                project_pixel_major(hp, [1])
+            for i in range(PAIR):
+                turn_edges(i)
+
+        def load_late(hp):
             if hp == 0:
                 load_scales(0, 1, 0, 6)
                 load_kind(2, 0)
@@ -358,10 +376,37 @@ def tile_relation_w_kernel(tc, x, w_qkv_words, w_qkv_scales, out):
             elif hp == 1:
                 for s in range(3):
                     load_kind(3, s)
+
+        for hp in range(pairs):
+            last = hp == pairs - 1
+            q[hp] = qkv.tile([P, 2, 2 * PAIR, PIXELS], BF16, name="q_halves", tag="q")
+            k[hp] = qkv.tile([P, 2, 2 * PAIR, EDGE + PIXELS], BF16, name="k_halves", tag="k")
+            v[hp] = qkv.tile([P, 2, TILES, PAIR_DIM], BF16, name="v_halves", tag="v")
+            for s in range(2):
+                if hp == 0:
+                    project_first(s)
+                else:
+                    for i in range(PAIR):
+                        project_channel_major(hp, s, i)
+            if hp > 0:
+                for i in range(PAIR):
+                    turn_tiles(hp - 1, i)
+            exps = attend(hp)
+            if last:
+                finish(exps)
             if hp > 0:
                 weighted_sum(hp - 1)
-            for i in range(PAIR):
-                transpose_weights(hp, i)
+            if last:
+                project_pixel_major(hp, 0)
+                project_pixel_major(hp, 1, 0, HEAD_DIM)
+                for i in range(PAIR):
+                    turn_tiles(hp, i)
+                project_pixel_major(hp, 1, HEAD_DIM, PAIR_DIM)
+            else:
+                project_pixel_major(hp, 0)
+                project_pixel_major(hp, 1)
+                finish(exps)
+            load_late(hp)
         weighted_sum(pairs - 1)
 
 
@@ -374,58 +419,74 @@ def quantise_x(nc, x_grouped, x_words, x_planes, g):
 
 
 def build_mask(nc, pool, cap, masked):
-    pix = pool.tile([P, 1], I32)
-    nc.gpsimd.iota(pix[:], pattern=[[0, 1]], base=0, channel_multiplier=1)
-    pix_row = pool.tile([P, 1], I32)
-    nc.vector.tensor_single_scalar(out=pix_row[:], in_=pix[:], scalar=4, op=ALU.arith_shift_right)
-    pix_col = pool.tile([P, 1], I32)
-    nc.vector.tensor_single_scalar(out=pix_col[:], in_=pix[:], scalar=SIDE - 1, op=ALU.bitwise_and)
-    key_row = pool.tile([P, BAND_ROWS, SIDE], F32)
+    pix = pool.tile([P, TILES], I32)
+    for t in range(TILES):
+        nc.gpsimd.iota(pix[:, t : t + 1], pattern=[[0, 1]], base=EDGE * t, channel_multiplier=1)
+    key_col = pool.tile([P, SIDE], F32)
     nc.gpsimd.iota(
-        key_row[:], pattern=[[1, BAND_ROWS], [0, SIDE]], base=0, channel_multiplier=0,
-        allow_small_or_imprecise_dtypes=True,
+        key_col[:], pattern=[[1, SIDE]], base=0, channel_multiplier=0, allow_small_or_imprecise_dtypes=True
     )
-    key_col = pool.tile([P, BAND_ROWS, SIDE], F32)
-    nc.gpsimd.iota(
-        key_col[:], pattern=[[0, BAND_ROWS], [1, SIDE]], base=0, channel_multiplier=0,
-        allow_small_or_imprecise_dtypes=True,
-    )
+    key_row = pool.tile([P, TILES, BAND_ROWS], F32)
+    for t in range(TILES):
+        lo = 0
+        for row, count in KEY_ROWS[t]:
+            nc.gpsimd.iota(
+                key_row[:, t, lo : lo + count], pattern=[[1, count]], base=row - TILE_ROWS * t,
+                channel_multiplier=0, allow_small_or_imprecise_dtypes=True,
+            )
+            lo += count
     slot = pool.tile([P, OUTSIDE], F32)
     nc.gpsimd.iota(
-        slot[:], pattern=[[1, OUTSIDE]], base=0, channel_multiplier=0,
-        allow_small_or_imprecise_dtypes=True,
+        slot[:], pattern=[[1, OUTSIDE]], base=0, channel_multiplier=0, allow_small_or_imprecise_dtypes=True
     )
+    row = pool.tile([P, TILES], I32)
+    nc.vector.tensor_single_scalar(out=row[:], in_=pix[:], scalar=4, op=ALU.arith_shift_right)
+    col = pool.tile([P, 1], I32)
+    nc.vector.tensor_single_scalar(out=col[:], in_=pix[:, 0:1], scalar=SIDE - 1, op=ALU.bitwise_and)
+    nc.vector.tensor_single_scalar(out=row[:], in_=row[:], scalar=TILE_ROWS - 1, op=ALU.bitwise_and)
     neg_col = pool.tile([P, 1], F32)
+    nc.vector.tensor_scalar(out=neg_col[:], in0=col[:], scalar1=-1.0, scalar2=None, op0=ALU.mult)
+    neg_row = pool.tile([P, TILES], F32)
+    nc.vector.tensor_scalar(out=neg_row[:], in0=row[:], scalar1=-1.0, scalar2=None, op0=ALU.mult)
+    col_dist = pool.tile([P, SIDE], F32)
     nc.vector.tensor_scalar(
-        out=neg_col[:], in0=pix_col[:], scalar1=-1.0, scalar2=None, op0=ALU.mult
+        out=col_dist[:], in0=key_col[:], scalar1=neg_col[:, 0:1], scalar2=None, op0=ALU.add
     )
-    col_dist = pool.tile([P, BAND], F32)
-    nc.scalar.activation(
-        out=col_dist[:], in_=key_col[:].rearrange("p r c -> p (r c)"), func=FUNC.Square,
-        bias=neg_col[:, 0:1], scale=1.0,
-    )
-    far = pool.tile([P, TILES, BAND], F32)
+    row_dist = pool.tile([P, TILES, BAND_ROWS], F32)
     for t in range(TILES):
-        neg_row = pool.tile([P, 1], F32, name="neg_row_%d" % t)
         nc.vector.tensor_scalar(
-            out=neg_row[:], in0=pix_row[:], scalar1=-1.0, scalar2=-float(REACH * t),
+            out=row_dist[:, t, :], in0=key_row[:, t, :], scalar1=neg_row[:, t : t + 1], scalar2=None,
+            op0=ALU.add,
+        )
+    squares, inside, caps = [], [], []
+    axes = (("col", [P, 1, SIDE], col_dist[:]), ("row", [P, TILES * BAND_ROWS, 1], row_dist[:].rearrange("p t r -> p (t r)")))
+    for name, shape, dist in axes:
+        squares.append(pool.tile([P, shape[1] * shape[2]], F32, name="square_" + name))
+        nc.vector.tensor_tensor(out=squares[-1][:], in0=dist, in1=dist, op=ALU.mult)
+    for n, (name, shape, dist) in enumerate(axes):
+        inside.append(pool.tile([P, shape[1] * shape[2]], F32, name="inside_" + name))
+        nc.vector.tensor_scalar(
+            out=inside[n][:], in0=squares[n][:], scalar1=REACH * REACH + 0.5, scalar2=None, op0=ALU.is_le
+        )
+    for n, (name, shape, dist) in enumerate(axes):
+        caps.append(pool.tile(shape, F32, name="cap_" + name))
+        nc.vector.tensor_scalar(
+            out=caps[n][:].rearrange("p a b -> p (a b)"), in0=inside[n][:], scalar1=2.0 * BIG, scalar2=-BIG,
             op0=ALU.mult, op1=ALU.add,
         )
-        row_dist = pool.tile([P, BAND], F32, name="row_dist_%d" % t)
-        nc.scalar.activation(
-            out=row_dist[:], in_=key_row[:].rearrange("p r c -> p (r c)"), func=FUNC.Square,
-            bias=neg_row[:, 0:1], scale=1.0,
-        )
-        nc.vector.tensor_tensor(out=far[:, t, :], in0=row_dist[:], in1=col_dist[:], op=ALU.max)
-    inside = pool.tile([P, TILES, BAND], F32)
-    nc.vector.tensor_scalar(
-        out=inside[:], in0=far[:], scalar1=REACH * REACH + 0.5, scalar2=None, op0=ALU.is_le
+    cols = pool.tile([P, 1], F32)
+    nc.vector.tensor_reduce(out=cols[:], in_=inside[0][:], axis=AXIS.X, op=ALU.add)
+    rows = pool.tile([P, TILES], F32)
+    nc.vector.tensor_reduce(
+        out=rows[:], in_=inside[1][:].rearrange("p (t r) -> p t r", t=TILES), axis=AXIS.X, op=ALU.add
     )
-    nc.vector.tensor_scalar(
-        out=cap[:], in0=inside[:], scalar1=2.0 * BIG, scalar2=-BIG, op0=ALU.mult, op1=ALU.add
+    whole = [P, TILES * BAND_ROWS, SIDE]
+    nc.vector.tensor_tensor(
+        out=cap[:].rearrange("p t (r c) -> p (t r) c", c=SIDE),
+        in0=caps[1][:].to_broadcast(whole), in1=caps[0][:].to_broadcast(whole), op=ALU.min,
     )
     count = pool.tile([P, TILES], F32)
-    nc.vector.tensor_reduce(out=count[:], in_=inside[:], axis=AXIS.X, op=ALU.add)
+    nc.vector.tensor_scalar(out=count[:], in0=rows[:], scalar1=cols[:, 0:1], scalar2=None, op0=ALU.mult)
     unused = pool.tile([P, TILES, OUTSIDE], F32)
     for t in range(TILES):
         nc.vector.tensor_scalar(

@@ -150,11 +150,13 @@ def tile_relation_w_kernel(tc, x, w_qkv_words, w_qkv_scales, out):
             for passes in FIRST_PIECES:
                 load_kind(0, 1, passes)
             load_scales(1, 0, 5, 8)
-            load_scales(2, 0, 0, 2)
-            load_kind(0, 2)
-            load_scales(2, 0, 2, 8)
-            for s in range(3):
-                load_kind(1, s)
+            load_kind(1, 0)
+            load_scales(2, 0, 0, 4)
+            for passes in FIRST_PIECES:
+                load_kind(1, 1, passes)
+            load_scales(2, 0, 4, 8)
+            for hp in range(2):
+                load_kind(hp, 2)
 
             x_grouped = setup.tile([P, PASSES, PIXELS, PACK], BF16, align_bytes=64)
             for g in range(PASSES):
@@ -189,31 +191,34 @@ def tile_relation_w_kernel(tc, x, w_qkv_words, w_qkv_scales, out):
             for halves, values in pieces:
                 nc.vector.tensor_tensor(out=halves[1], in0=values, in1=halves[0], op=ALU.subtract)
 
-        def project_first(s):
+        def project_open(hp, s):
             banks = [ps_att.tile([P, PIXELS], F32, name="bank_%d" % c, tag="att") for c in range(2 * PAIR)]
+            plane_lo = (hp % 2) * PAIR_DIM
             for passes in FIRST_PIECES:
                 for c in range(2 * PAIR):
                     for g in range(passes.start, passes.stop):
                         nc.tensor.matmul_mx(
                             out=banks[c][:],
-                            lhsT=w_words[0][s][:, g, P * c : P * (c + 1)].bitcast(FP8X4),
-                            lhsT_scale=w_planes[s][0][plane_rows(g), plane_slot(g), P * c : P * (c + 1)],
+                            lhsT=w_words[hp % 2][s][:, g, P * c : P * (c + 1)].bitcast(FP8X4),
+                            lhsT_scale=w_planes[s][hp // 2][
+                                plane_rows(g), plane_slot(g), plane_lo + P * c : plane_lo + P * (c + 1)
+                            ],
                             rhs=x_words[:, g, :].bitcast(FP8X4),
                             rhs_scale=x_planes[:, g, :],
                             start=(g == 0),
                             stop=(g == PASSES - 1),
                         )
             for c in range(2 * PAIR):
-                if c < 2:
+                if hp == 0 and c < 2:
                     nc.scalar.copy(out=whole[s][:, c, EDGE * s : EDGE * s + PIXELS], in_=banks[c][:])
                     if s == 1:
                         nc.scalar.copy(out=whole[1][:, c, 0:EDGE], in_=banks[c][:, PIXELS - EDGE : PIXELS])
                 elif s == 0:
-                    split([q[0][:, a, c, :] for a in range(2)], banks[c][:])
+                    split([q[hp][:, a, c, :] for a in range(2)], banks[c][:])
                 else:
                     split(
-                        [k[0][:, a, c, EDGE : EDGE + PIXELS] for a in range(2)], banks[c][:],
-                        [k[0][:, a, c, 0:EDGE] for a in range(2)], banks[c][:, PIXELS - EDGE : PIXELS],
+                        [k[hp][:, a, c, EDGE : EDGE + PIXELS] for a in range(2)], banks[c][:],
+                        [k[hp][:, a, c, 0:EDGE] for a in range(2)], banks[c][:, PIXELS - EDGE : PIXELS],
                     )
 
         def project_channel_major(hp, s, i):
@@ -383,30 +388,44 @@ def tile_relation_w_kernel(tc, x, w_qkv_words, w_qkv_scales, out):
             k[hp] = qkv.tile([P, 2, 2 * PAIR, EDGE + PIXELS], BF16, name="k_halves", tag="k")
             v[hp] = qkv.tile([P, 2, TILES, PAIR_DIM], BF16, name="v_halves", tag="v")
             for s in range(2):
-                if hp == 0:
-                    project_first(s)
+                if hp == 0 or (hp == 1 and s == 1):
+                    project_open(hp, s)
                 else:
                     for i in range(PAIR):
                         project_channel_major(hp, s, i)
-            if hp > 0:
-                for i in range(PAIR):
-                    turn_tiles(hp - 1, i)
-            exps = attend(hp)
-            if last:
+            if hp == 0:
+                exps = attend(hp)
                 finish(exps)
-            if hp > 0:
-                weighted_sum(hp - 1)
-            if last:
+            elif hp == 1:
+                for i in range(PAIR):
+                    turn_tiles(0, i)
+                exps = attend(hp)
+                for u in range(2):
+                    for t in range(TILES):
+                        project_pixel_major(u, t)
+                    if u == 0:
+                        finish(exps)
+                    load_late(u)
+                for i in range(PAIR):
+                    turn_tiles(1, i)
+                weighted_sum(0)
+                weighted_sum(1)
+            elif hp == 2:
+                project_pixel_major(hp, 0)
+                exps = attend(hp)
+                project_pixel_major(hp, 1)
+                finish(exps)
+            else:
+                for i in range(PAIR):
+                    turn_tiles(2, i)
+                exps = attend(hp)
+                finish(exps)
+                weighted_sum(2)
                 project_pixel_major(hp, 0)
                 project_pixel_major(hp, 1, 0, HEAD_DIM)
                 for i in range(PAIR):
                     turn_tiles(hp, i)
                 project_pixel_major(hp, 1, HEAD_DIM, PAIR_DIM)
-            else:
-                project_pixel_major(hp, 0)
-                project_pixel_major(hp, 1)
-                finish(exps)
-            load_late(hp)
         weighted_sum(pairs - 1)
 
 

@@ -35,8 +35,10 @@ PAIR = 2
 PAIR_DIM = PAIR * HEAD_DIM
 PLANES_PER_TILE = 4
 PLANE_SLOTS = 2
+SCALE_DMAS = 4 * PLANE_SLOTS
 WARM_PASSES = 16
-FIRST_PIECES = (slice(0, PASSES // 2), slice(PASSES // 2, PASSES))
+HALVES = (slice(0, PASSES // 2), slice(PASSES // 2, PASSES))
+IN_HALVES = ((0, 0), (0, 1), (1, 1))
 BIG = 1.0e30
 PRODUCTS = ((0, 0), (1, 0), (0, 1))
 
@@ -114,12 +116,13 @@ def tile_relation_w_kernel(tc, x, w_qkv_words, w_qkv_scales, out):
                     ].bitcast(I32),
                 )
 
-        def load_kind(hp, s, passes=slice(0, PASSES)):
+        def load_words(hp, s):
             first = PACK * (s * D + hp * PAIR_DIM)
-            nc.sync.dma_start(
-                out=w_words[hp % 2][s][:, passes, :].bitcast(I32),
-                in_=w_bytes[:, passes, first : first + PACK * PAIR_DIM].bitcast(I32),
-            )
+            for passes in HALVES if (hp, s) in IN_HALVES else (slice(0, PASSES),):
+                nc.sync.dma_start(
+                    out=w_words[hp % 2][s][:, passes, :].bitcast(I32),
+                    in_=w_bytes[:, passes, first : first + PACK * PAIR_DIM].bitcast(I32),
+                )
 
         ps_proj = stack.enter_context(tc.psum_pool(name="ps_proj", bufs=3))
         ps_att = stack.enter_context(tc.psum_pool(name="ps_att", bufs=5))
@@ -143,20 +146,17 @@ def tile_relation_w_kernel(tc, x, w_qkv_words, w_qkv_scales, out):
                 nc.sync.dma_start(out=x_raw[:, g : g + 2], in_=x_rows[:, g : g + 2])
                 if g == 0:
                     load_scales(0, 0, 0, 4)
-            load_scales(0, 0, 4, 8)
-            for passes in FIRST_PIECES:
-                load_kind(0, 0, passes)
+            load_scales(0, 0, 4, SCALE_DMAS)
+            load_words(0, 0)
             load_scales(1, 0, 0, 5)
-            for passes in FIRST_PIECES:
-                load_kind(0, 1, passes)
-            load_scales(1, 0, 5, 8)
-            load_kind(1, 0)
+            load_words(0, 1)
+            load_scales(1, 0, 5, SCALE_DMAS)
+            load_words(1, 0)
             load_scales(2, 0, 0, 4)
-            for passes in FIRST_PIECES:
-                load_kind(1, 1, passes)
-            load_scales(2, 0, 4, 8)
-            for hp in range(2):
-                load_kind(hp, 2)
+            load_words(1, 1)
+            load_scales(2, 0, 4, SCALE_DMAS)
+            load_words(0, 2)
+            load_words(1, 2)
 
             x_grouped = setup.tile([P, PASSES, PIXELS, PACK], BF16, align_bytes=64)
             for g in range(PASSES):
@@ -191,10 +191,16 @@ def tile_relation_w_kernel(tc, x, w_qkv_words, w_qkv_scales, out):
             for halves, values in pieces:
                 nc.vector.tensor_tensor(out=halves[1], in0=values, in1=halves[0], op=ALU.subtract)
 
-        def project_open(hp, s):
+        def store_k(hp, chans, bank, rows_8_9):
+            split(
+                [k[hp][:, a, chans, EDGE : EDGE + PIXELS] for a in range(2)], bank,
+                [k[hp][:, a, chans, 0:EDGE] for a in range(2)], rows_8_9,
+            )
+
+        def project_in_halves(hp, s):
             banks = [ps_att.tile([P, PIXELS], F32, name="bank_%d" % c, tag="att") for c in range(2 * PAIR)]
             plane_lo = (hp % 2) * PAIR_DIM
-            for passes in FIRST_PIECES:
+            for passes in HALVES:
                 for c in range(2 * PAIR):
                     for g in range(passes.start, passes.stop):
                         nc.tensor.matmul_mx(
@@ -216,20 +222,17 @@ def tile_relation_w_kernel(tc, x, w_qkv_words, w_qkv_scales, out):
                 elif s == 0:
                     split([q[hp][:, a, c, :] for a in range(2)], banks[c][:])
                 else:
-                    split(
-                        [k[hp][:, a, c, EDGE : EDGE + PIXELS] for a in range(2)], banks[c][:],
-                        [k[hp][:, a, c, 0:EDGE] for a in range(2)], banks[c][:, PIXELS - EDGE : PIXELS],
-                    )
+                    store_k(hp, c, banks[c][:], banks[c][:, PIXELS - EDGE : PIXELS])
 
-        def project_channel_major(hp, s, i):
+        def project_head(hp, s, i):
             bank = ps_proj.tile([P, 2, PIXELS], F32, tag="proj")
             for c in range(2):
-                words, lo = w_words[hp % 2][s], HEAD_DIM * i + P * c
-                plane_lo = (hp % 2) * PAIR_DIM + HEAD_DIM * i + P * c
+                lo = HEAD_DIM * i + P * c
+                plane_lo = (hp % 2) * PAIR_DIM + lo
                 for g in range(PASSES):
                     nc.tensor.matmul_mx(
                         out=bank[:, c, :],
-                        lhsT=words[:, g, lo : lo + P].bitcast(FP8X4),
+                        lhsT=w_words[hp % 2][s][:, g, lo : lo + P].bitcast(FP8X4),
                         lhsT_scale=w_planes[s][hp // 2][plane_rows(g), plane_slot(g), plane_lo : plane_lo + P],
                         rhs=x_words[:, g, :].bitcast(FP8X4),
                         rhs_scale=x_planes[:, g, :],
@@ -237,33 +240,26 @@ def tile_relation_w_kernel(tc, x, w_qkv_words, w_qkv_scales, out):
                         stop=(g == PASSES - 1),
                     )
             chans = slice(2 * i, 2 * i + 2)
-            if hp == 0 and i == 0:
-                nc.scalar.copy(out=whole[s][:, :, EDGE * s : EDGE * s + PIXELS], in_=bank[:])
-                if s == 1:
-                    nc.scalar.copy(out=whole[1][:, :, 0:EDGE], in_=bank[:, :, PIXELS - EDGE : PIXELS])
-            elif s == 0:
+            if s == 0:
                 split([q[hp][:, a, chans, :] for a in range(2)], bank[:])
             else:
-                split(
-                    [k[hp][:, a, chans, EDGE : EDGE + PIXELS] for a in range(2)], bank[:],
-                    [k[hp][:, a, chans, 0:EDGE] for a in range(2)], bank[:, :, PIXELS - EDGE : PIXELS],
-                )
+                store_k(hp, chans, bank[:], bank[:, :, PIXELS - EDGE : PIXELS])
 
-        def project_pixel_major(hp, t, lo=0, hi=PAIR_DIM):
-            plane_cols = slice((hp % 2) * PAIR_DIM + lo, (hp % 2) * PAIR_DIM + hi)
-            bank = ps_proj.tile([P, hi - lo], F32, name="v_bank", tag="proj")
+        def project_tile(hp, t):
+            plane_cols = slice((hp % 2) * PAIR_DIM, (hp % 2 + 1) * PAIR_DIM)
+            bank = ps_proj.tile([P, PAIR_DIM], F32, name="v_bank", tag="proj")
             pix = slice(P * t, P * (t + 1))
             for g in range(PASSES):
                 nc.tensor.matmul_mx(
                     out=bank[:],
                     lhsT=x_words[:, g, pix].bitcast(FP8X4),
                     lhsT_scale=x_planes[:, g, pix],
-                    rhs=w_words[hp % 2][2][:, g, lo:hi].bitcast(FP8X4),
+                    rhs=w_words[hp % 2][2][:, g, :].bitcast(FP8X4),
                     rhs_scale=w_planes[2][hp // 2][plane_rows(g), plane_slot(g), plane_cols],
                     start=(g == 0),
                     stop=(g == PASSES - 1),
                 )
-            split([v[hp][:, a, t, lo:hi] for a in range(2)], bank[:])
+            split([v[hp][:, a, t, :] for a in range(2)], bank[:])
 
         def scores(hp, i):
             score = ps_att.tile([P, TILES, BAND], F32, tag="att")
@@ -314,27 +310,25 @@ def tile_relation_w_kernel(tc, x, w_qkv_words, w_qkv_scales, out):
                     op0=ALU.mult,
                 )
 
-        edges = {}
-
-        def turn_edges(i):
-            edges[i] = work.tile([P, TILES, EDGE], F32, name="edge_%d" % i, tag="edge_%d" % i, align_bytes=64)
+        def turn_edges(hp, i):
+            edge = work.tile([P, TILES, EDGE], F32, name="edge_%d" % i, tag="edge_%d" % i, align_bytes=64)
             for t in range(TILES):
-                nc.vector.transpose(out=edges[i][:, 1 - t, :], in_=att[i][:, t, 0:EDGE])
+                nc.vector.transpose(out=edge[:, 1 - t, :], in_=att[i][:, t, 0:EDGE])
+            att_t[(hp, i)] = work.tile([P, 2, TILES, BAND], BF16, name="att_t_%d" % i, tag="att_t_%d" % i)
+            hi, lo = [att_t[(hp, i)][:, a, :, 0:EDGE] for a in range(2)]
+            nc.gpsimd.tensor_copy(out=hi, in_=edge[:])
+            nc.gpsimd.tensor_tensor(out=lo, in0=edge[:], in1=hi, op=ALU.subtract)
 
         def turn_tiles(hp, i):
             bank = ps_att.tile([P, TILES, P], F32, name="own", tag="att")
             for t in range(TILES):
                 nc.tensor.transpose(out=bank[:, t, :], in_=att[i][:, t, EDGE:BAND], identity=ident[:])
-            att_t[(hp, i)] = work.tile([P, 2, TILES, BAND], BF16, name="att_t_%d" % i, tag="att_t_%d" % i)
-            split(
-                [att_t[(hp, i)][:, a, :, EDGE:BAND] for a in range(2)], bank[:],
-                [att_t[(hp, i)][:, a, :, 0:EDGE] for a in range(2)], edges[i][:],
-            )
+            split([att_t[(hp, i)][:, a, :, EDGE:BAND] for a in range(2)], bank[:])
 
         def weighted_sum(hp):
             res = [results.tile([P, 2, PIXELS], F32, name="res_%d" % i, tag="res") for i in range(PAIR)]
-            for j in range(TILES):
-                for i in range(PAIR):
+            for i in range(PAIR):
+                for j in range(TILES):
                     part = ps_att.tile([P, 2, BAND], F32, name="part", tag="att")
                     for c in range(2):
                         chan = slice(HEAD_DIM * i + P * c, HEAD_DIM * i + P * (c + 1))
@@ -352,7 +346,8 @@ def tile_relation_w_kernel(tc, x, w_qkv_words, w_qkv_scales, out):
                     else:
                         nc.scalar.copy(out=res[i][:, :, P + EDGE : PIXELS], in_=part[:, :, EDGE:P])
                         both = res[i][:, :, P - EDGE : P + EDGE].rearrange("p c (s w) -> p c s w", w=EDGE)
-                        ends = part[:].rearrange("p c (s w) -> p c s w", w=EDGE)[:, :, 0 : BAND_ROWS // REACH : P // EDGE, :]
+                        runs = part[:].rearrange("p c (s w) -> p c s w", w=EDGE)
+                        ends = runs[:, :, 0 : BAND // EDGE : BAND // EDGE - 1, :]
                         nc.vector.tensor_tensor(out=both, in0=both, in1=ends, op=ALU.add)
                         head = PAIR * hp + i
                         nc.sync.dma_start(out=out_rows[:, 2 * head : 2 * head + 2, :], in_=res[i][:])
@@ -361,72 +356,71 @@ def tile_relation_w_kernel(tc, x, w_qkv_words, w_qkv_scales, out):
             neg_max = [scores(hp, i) for i in range(PAIR)]
             return [exponentials(i, neg_max[i]) for i in range(PAIR)]
 
-        def finish(exps):
+        def finish(hp, exps):
             for i in range(PAIR):
                 normalise(i, exps[i][0], exps[i][1])
             for i in range(PAIR):
-                turn_edges(i)
+                turn_edges(hp, i)
 
-        def load_late(hp):
-            if hp == 0:
-                load_scales(0, 1, 0, 6)
-                load_kind(2, 0)
-                load_scales(0, 1, 6, 8)
-                load_scales(1, 1, 0, 4)
-                load_kind(2, 1)
-                load_scales(1, 1, 4, 8)
-                load_scales(2, 1, 0, 2)
-                load_kind(2, 2)
-                load_scales(2, 1, 2, 8)
-            elif hp == 1:
-                for s in range(3):
-                    load_kind(3, s)
-
-        for hp in range(pairs):
-            last = hp == pairs - 1
-            q[hp] = qkv.tile([P, 2, 2 * PAIR, PIXELS], BF16, name="q_halves", tag="q")
-            k[hp] = qkv.tile([P, 2, 2 * PAIR, EDGE + PIXELS], BF16, name="k_halves", tag="k")
-            v[hp] = qkv.tile([P, 2, TILES, PAIR_DIM], BF16, name="v_halves", tag="v")
-            for s in range(2):
-                if hp == 0 or (hp == 1 and s == 1):
-                    project_open(hp, s)
-                else:
-                    for i in range(PAIR):
-                        project_channel_major(hp, s, i)
-            if hp == 0:
-                exps = attend(hp)
-                finish(exps)
-            elif hp == 1:
-                for i in range(PAIR):
-                    turn_tiles(0, i)
-                exps = attend(hp)
-                for u in range(2):
-                    for t in range(TILES):
-                        project_pixel_major(u, t)
-                    if u == 0:
-                        finish(exps)
-                    load_late(u)
-                for i in range(PAIR):
-                    turn_tiles(1, i)
-                weighted_sum(0)
-                weighted_sum(1)
-            elif hp == 2:
-                project_pixel_major(hp, 0)
-                exps = attend(hp)
-                project_pixel_major(hp, 1)
-                finish(exps)
+        def project(hp, s):
+            if s == 0:
+                q[hp] = qkv.tile([P, 2, 2 * PAIR, PIXELS], BF16, name="q_halves", tag="q")
+            elif s == 1:
+                k[hp] = qkv.tile([P, 2, 2 * PAIR, EDGE + PIXELS], BF16, name="k_halves", tag="k")
             else:
+                v[hp] = qkv.tile([P, 2, TILES, PAIR_DIM], BF16, name="v_halves", tag="v")
+            if (hp, s) in IN_HALVES:
+                project_in_halves(hp, s)
+            elif s < 2:
                 for i in range(PAIR):
-                    turn_tiles(2, i)
-                exps = attend(hp)
-                finish(exps)
-                weighted_sum(2)
-                project_pixel_major(hp, 0)
-                project_pixel_major(hp, 1, 0, HEAD_DIM)
-                for i in range(PAIR):
-                    turn_tiles(hp, i)
-                project_pixel_major(hp, 1, HEAD_DIM, PAIR_DIM)
-        weighted_sum(pairs - 1)
+                    project_head(hp, s, i)
+            else:
+                for t in range(TILES):
+                    project_tile(hp, t)
+
+        def turn(hp):
+            for i in range(PAIR):
+                turn_tiles(hp, i)
+
+        project(0, 0)
+        project(0, 1)
+        finish(0, attend(0))
+        project(1, 0)
+        project(1, 1)
+        turn(0)
+        exps = attend(1)
+        project(0, 2)
+        finish(1, exps)
+        load_scales(0, 1, 0, 6)
+        load_words(2, 0)
+        load_scales(0, 1, 6, SCALE_DMAS)
+        load_scales(1, 1, 0, 4)
+        load_words(2, 1)
+        load_scales(1, 1, 4, SCALE_DMAS)
+        project(1, 2)
+        load_words(3, 0)
+        load_scales(2, 1, 0, 4)
+        load_words(3, 1)
+        load_scales(2, 1, 4, SCALE_DMAS)
+        load_words(2, 2)
+        load_words(3, 2)
+        turn(1)
+        weighted_sum(0)
+        weighted_sum(1)
+
+        project(2, 0)
+        project(2, 1)
+        project(3, 0)
+        finish(2, attend(2))
+        project(3, 1)
+        turn(2)
+        exps = attend(3)
+        project(2, 2)
+        finish(3, exps)
+        project(3, 2)
+        turn(3)
+        weighted_sum(2)
+        weighted_sum(3)
 
 
 def quantise_x(nc, x_grouped, x_words, x_planes, g):

@@ -310,57 +310,61 @@ def tile_relation_w_kernel(tc, x, w_qkv_words, w_qkv_scales, out):
                     op0=ALU.mult,
                 )
 
-        def turn_edges(hp, i):
-            edge = work.tile([P, TILES, EDGE], F32, name="edge_%d" % i, tag="edge_%d" % i, align_bytes=64)
+        edges = {}
+
+        def turn_edges(i):
+            edges[i] = work.tile([P, TILES, EDGE], F32, name="edge_%d" % i, tag="edge_%d" % i, align_bytes=64)
             for t in range(TILES):
-                nc.vector.transpose(out=edge[:, 1 - t, :], in_=att[i][:, t, 0:EDGE])
-            att_t[(hp, i)] = work.tile([P, 2, TILES, BAND], BF16, name="att_t_%d" % i, tag="att_t_%d" % i)
-            hi, lo = [att_t[(hp, i)][:, a, :, 0:EDGE] for a in range(2)]
-            nc.gpsimd.tensor_copy(out=hi, in_=edge[:])
-            nc.gpsimd.tensor_tensor(out=lo, in0=edge[:], in1=hi, op=ALU.subtract)
+                nc.vector.transpose(out=edges[i][:, 1 - t, :], in_=att[i][:, t, 0:EDGE])
 
         def turn_tiles(hp, i):
             bank = ps_att.tile([P, TILES, P], F32, name="own", tag="att")
             for t in range(TILES):
                 nc.tensor.transpose(out=bank[:, t, :], in_=att[i][:, t, EDGE:BAND], identity=ident[:])
-            split([att_t[(hp, i)][:, a, :, EDGE:BAND] for a in range(2)], bank[:])
+            att_t[(hp, i)] = work.tile([P, 2, TILES, BAND], BF16, name="att_t_%d" % i, tag="att_t_%d" % i)
+            split(
+                [att_t[(hp, i)][:, a, :, EDGE:BAND] for a in range(2)], bank[:],
+                [att_t[(hp, i)][:, a, :, 0:EDGE] for a in range(2)], edges[i][:],
+            )
 
         def weighted_sum(hp):
             res = [results.tile([P, 2, PIXELS], F32, name="res_%d" % i, tag="res") for i in range(PAIR)]
             for i in range(PAIR):
-                for j in range(TILES):
-                    part = ps_att.tile([P, 2, BAND], F32, name="part", tag="att")
-                    for c in range(2):
+                head = PAIR * hp + i
+                steps = ((0, 0, 2), (1, 0, 2)) if head < HEADS - 1 else ((0, 0, 2), (1, 0, 1), (1, 1, 2))
+                for j, lo, hi in steps:
+                    part = ps_att.tile([P, hi - lo, BAND], F32, name="part", tag="att")
+                    for c in range(lo, hi):
                         chan = slice(HEAD_DIM * i + P * c, HEAD_DIM * i + P * (c + 1))
                         for n, (a, b) in enumerate(PRODUCTS):
                             nc.tensor.matmul(
-                                out=part[:, c, :],
+                                out=part[:, c - lo, :],
                                 lhsT=v[hp][:, a, j, chan],
                                 rhs=att_t[(hp, i)][:, b, j, :],
                                 start=(n == 0),
                                 stop=(n == len(PRODUCTS) - 1),
                             )
+                    dest = res[i][:, lo:hi, :]
                     if j == 0:
-                        nc.scalar.copy(out=res[i][:, :, P : P + EDGE], in_=part[:, :, 0:EDGE])
-                        nc.vector.tensor_copy(out=res[i][:, :, 0:P], in_=part[:, :, EDGE:BAND])
+                        nc.scalar.copy(out=dest[:, :, P : P + EDGE], in_=part[:, :, 0:EDGE])
+                        nc.vector.tensor_copy(out=dest[:, :, 0:P], in_=part[:, :, EDGE:BAND])
                     else:
-                        nc.scalar.copy(out=res[i][:, :, P + EDGE : PIXELS], in_=part[:, :, EDGE:P])
-                        both = res[i][:, :, P - EDGE : P + EDGE].rearrange("p c (s w) -> p c s w", w=EDGE)
+                        nc.scalar.copy(out=dest[:, :, P + EDGE : PIXELS], in_=part[:, :, EDGE:P])
+                        both = dest[:, :, P - EDGE : P + EDGE].rearrange("p c (s w) -> p c s w", w=EDGE)
                         runs = part[:].rearrange("p c (s w) -> p c s w", w=EDGE)
                         ends = runs[:, :, 0 : BAND // EDGE : BAND // EDGE - 1, :]
                         nc.vector.tensor_tensor(out=both, in0=both, in1=ends, op=ALU.add)
-                        head = PAIR * hp + i
-                        nc.sync.dma_start(out=out_rows[:, 2 * head : 2 * head + 2, :], in_=res[i][:])
+                        nc.sync.dma_start(out=out_rows[:, 2 * head + lo : 2 * head + hi, :], in_=dest)
 
         def attend(hp):
             neg_max = [scores(hp, i) for i in range(PAIR)]
             return [exponentials(i, neg_max[i]) for i in range(PAIR)]
 
-        def finish(hp, exps):
+        def finish(exps):
             for i in range(PAIR):
                 normalise(i, exps[i][0], exps[i][1])
             for i in range(PAIR):
-                turn_edges(hp, i)
+                turn_edges(i)
 
         def project(hp, s):
             if s == 0:
@@ -384,13 +388,13 @@ def tile_relation_w_kernel(tc, x, w_qkv_words, w_qkv_scales, out):
 
         project(0, 0)
         project(0, 1)
-        finish(0, attend(0))
+        finish(attend(0))
         project(1, 0)
         project(1, 1)
         turn(0)
         exps = attend(1)
         project(0, 2)
-        finish(1, exps)
+        finish(exps)
         load_scales(0, 1, 0, 6)
         load_words(2, 0)
         load_scales(0, 1, 6, SCALE_DMAS)
@@ -411,12 +415,12 @@ def tile_relation_w_kernel(tc, x, w_qkv_words, w_qkv_scales, out):
         project(2, 0)
         project(2, 1)
         project(3, 0)
-        finish(2, attend(2))
+        finish(attend(2))
         project(3, 1)
         turn(2)
         exps = attend(3)
         project(2, 2)
-        finish(3, exps)
+        finish(exps)
         project(3, 2)
         turn(3)
         weighted_sum(2)

from contextlib import ExitStack

import concourse.mybir as mybir
from concourse.masks import make_identity

F32 = mybir.dt.float32
BF16 = mybir.dt.bfloat16
I32 = mybir.dt.int32
U32 = mybir.dt.uint32
U8 = mybir.dt.uint8
FP8X4 = mybir.dt.float8_e4m3fn_x4
ALU = mybir.AluOpType
FUNC = mybir.ActivationFunctionType
AXIS = mybir.AxisListType

P = 128
PACK = 4
C_IN = 3072
PASSES = C_IN // (P * PACK)
D = 2048
HEADS = 8
HEAD_DIM = D // HEADS
SIDE = 16
PIXELS = SIDE * SIDE
REACH = 2
WINDOW = (2 * REACH + 1) ** 2
TILES = PIXELS // P
TILE_ROWS = P // SIDE
BAND_ROWS = TILE_ROWS + REACH
BAND = BAND_ROWS * SIDE
EDGE = REACH * SIDE
KEY_ROWS = (((8, 2), (0, 8)), ((6, 2), (10, 6), (8, 2)))
OUTSIDE = WINDOW - (REACH + 1) ** 2
PAIR = 2
PAIR_DIM = PAIR * HEAD_DIM
PLANES_PER_TILE = 4
PLANE_SLOTS = 2
SCALE_DMAS = 4 * PLANE_SLOTS
WARM_PASSES = 16
HALVES = (slice(0, PASSES // 2), slice(PASSES // 2, PASSES))
IN_HALVES = ((0, 0), (0, 1), (1, 1))
BIG = 1.0e30
PRODUCTS = ((0, 0), (1, 0), (0, 1))

FLOPS = 2 * 3 * D * C_IN * PIXELS + 2 * 2 * D * WINDOW * PIXELS


def band(t):
    return slice(P * t, P * t + BAND)


def plane_rows(g):
    return slice(PACK * (g % PLANES_PER_TILE), P)


def plane_slot(g):
    return g // PLANES_PER_TILE


def tile_relation_w_kernel(tc, x, w_qkv_words, w_qkv_scales, out):
    nc = tc.nc
    pairs = HEADS // PAIR

    x_rows = x[0].rearrange("(g p t) h w -> p g t (h w)", g=PASSES, p=P, t=PACK)
    w_bytes = w_qkv_words.rearrange("g p n t -> p g (n t)")
    out_rows = out[0].rearrange("(a p) h w -> p a (h w)", p=P)

    with ExitStack() as stack:
        stack.enter_context(tc.manual_schedule())
        keep = stack.enter_context(tc.tile_pool(name="keep", bufs=1))

        w_words = [
            [
                keep.tile([P, PASSES, PAIR_DIM], U32, name="w_words_%d_%d" % (b, s), align_bytes=64)
                for s in range(3)
            ]
            for b in range(2)
        ]
        w_planes = [
            [
                keep.tile([P, PLANE_SLOTS, 2 * PAIR_DIM], U8, name="w_planes_%d_%d" % (s, b), align_bytes=64)
                for b in range(pairs // 2)
            ]
            for s in range(3)
        ]
        x_words = keep.tile([P, PASSES, PIXELS], U32, align_bytes=64)
        x_planes = keep.tile([P, PASSES, PIXELS], U8, align_bytes=64)
        ident = keep.tile([P, P], F32)
        cap = keep.tile([P, TILES, BAND], F32)
        masked = [
            keep.tile([P, TILES, BAND + OUTSIDE], F32, name="masked_%d" % i) for i in range(PAIR)
        ]
        att = [keep.tile([P, TILES, BAND], F32, name="att_%d" % i, align_bytes=64) for i in range(PAIR)]
        warm = keep.tile([P, 1], F32)

        nc.vector.memset(w_planes[0][0][:].bitcast(I32), 0)
        nc.vector.memset(warm[:], 0.0)
        nc.scalar.activation(out=warm[:], in_=warm[:], func=FUNC.Exp)
        mask_pool = stack.enter_context(tc.tile_pool(name="mask_pool", bufs=1))
        build_mask(nc, mask_pool, cap, masked)
        for s in (1, 2):
            nc.gpsimd.memset(w_planes[s][0][:].bitcast(I32), 0)
        make_identity(nc, ident[:])

        def load_scales(s, b, first, last):
            lo = s * D + b * 2 * PAIR_DIM
            for n in range(first, last):
                slot, quad = divmod(n, 4)
                g_lo = slot * PLANES_PER_TILE
                g_hi = min(g_lo + PLANES_PER_TILE, PASSES)
                rows = slice(32 * quad, 32 * quad + PACK * (g_hi - g_lo))
                nc.sync.dma_start(
                    out=w_planes[s][b][rows, slot, :].bitcast(I32),
                    in_=w_qkv_scales[
                        g_lo:g_hi, PACK * quad : PACK * (quad + 1), lo : lo + 2 * PAIR_DIM
                    ].bitcast(I32),
                )

        def load_words(hp, s):
            first = PACK * (s * D + hp * PAIR_DIM)
            for passes in HALVES if (hp, s) in IN_HALVES else (slice(0, PASSES),):
                nc.sync.dma_start(
                    out=w_words[hp % 2][s][:, passes, :].bitcast(I32),
                    in_=w_bytes[:, passes, first : first + PACK * PAIR_DIM].bitcast(I32),
                )

        ps_proj = stack.enter_context(tc.psum_pool(name="ps_proj", bufs=3))
        ps_att = stack.enter_context(tc.psum_pool(name="ps_att", bufs=5))

        def warm_up():
            bank = ps_att.tile([P, PIXELS], F32, name="warm_bank", tag="att")
            for n in range(WARM_PASSES):
                nc.tensor.matmul_mx(
                    out=bank[:],
                    lhsT=x_words[:, 0, 0:P].bitcast(FP8X4),
                    lhsT_scale=x_planes[:, 0, 0:P],
                    rhs=x_words[:, 0, :].bitcast(FP8X4),
                    rhs_scale=x_planes[:, 0, :],
                    start=(n == 0),
                    stop=(n == WARM_PASSES - 1),
                )

        with tc.tile_pool(name="setup", bufs=1) as setup:
            x_raw = setup.tile([P, PASSES, PACK, PIXELS], BF16)
            for g in range(0, PASSES, 2):
                nc.sync.dma_start(out=x_raw[:, g : g + 2], in_=x_rows[:, g : g + 2])
                if g == 0:
                    load_scales(0, 0, 0, 4)
            load_scales(0, 0, 4, SCALE_DMAS)
            load_words(0, 0)
            load_scales(1, 0, 0, 5)
            load_words(0, 1)
            load_scales(1, 0, 5, SCALE_DMAS)
            load_words(1, 0)
            load_scales(2, 0, 0, 4)
            load_words(1, 1)
            load_scales(2, 0, 4, SCALE_DMAS)
            load_words(0, 2)
            load_words(1, 2)

            x_grouped = setup.tile([P, PASSES, PIXELS, PACK], BF16, align_bytes=64)
            for g in range(PASSES):
                rows = x_raw[:, g].rearrange("p t n -> p n t")
                nc.scalar.copy(out=x_grouped[:, g, 0:P, :], in_=rows[:, 0:P, :])
                nc.vector.tensor_copy(out=x_grouped[:, g, P : PIXELS - EDGE, :], in_=rows[:, P + EDGE : PIXELS, :])
                nc.scalar.copy(out=x_grouped[:, g, PIXELS - EDGE : PIXELS, :], in_=rows[:, P : P + EDGE, :])
                if g > 0:
                    quantise_x(nc, x_grouped, x_words, x_planes, g - 1)
                if g == 1:
                    warm_up()
            quantise_x(nc, x_grouped, x_words, x_planes, PASSES - 1)

        for s in range(3):
            nc.vector.memset(w_planes[s][1][:].bitcast(I32), 0)

        qkv = stack.enter_context(tc.tile_pool(name="qkv", bufs=2))
        work = stack.enter_context(tc.tile_pool(name="work", bufs=2))
        small = stack.enter_context(tc.tile_pool(name="small", bufs=4))
        results = stack.enter_context(tc.tile_pool(name="results", bufs=HEADS))

        q, k, v, att_t = {}, {}, {}, {}
        whole = [
            qkv.tile([P, 2, PIXELS + EDGE * s], F32, name="whole_%d" % s, tag="whole_%d" % s, bufs=1)
            for s in range(2)
        ]

        def split(*pieces):
            pieces = list(zip(pieces[0::2], pieces[1::2]))
            for halves, values in pieces:
                nc.scalar.copy(out=halves[0], in_=values)
            for halves, values in pieces:
                nc.vector.tensor_tensor(out=halves[1], in0=values, in1=halves[0], op=ALU.subtract)

        def store_k(hp, chans, bank, rows_8_9):
            split(
                [k[hp][:, a, chans, EDGE : EDGE + PIXELS] for a in range(2)], bank,
                [k[hp][:, a, chans, 0:EDGE] for a in range(2)], rows_8_9,
            )

        def project_in_halves(hp, s):
            banks = [ps_att.tile([P, PIXELS], F32, name="bank_%d" % c, tag="att") for c in range(2 * PAIR)]
            plane_lo = (hp % 2) * PAIR_DIM
            for passes in HALVES:
                for c in range(2 * PAIR):
                    for g in range(passes.start, passes.stop):
                        nc.tensor.matmul_mx(
                            out=banks[c][:],
                            lhsT=w_words[hp % 2][s][:, g, P * c : P * (c + 1)].bitcast(FP8X4),
                            lhsT_scale=w_planes[s][hp // 2][
                                plane_rows(g), plane_slot(g), plane_lo + P * c : plane_lo + P * (c + 1)
                            ],
                            rhs=x_words[:, g, :].bitcast(FP8X4),
                            rhs_scale=x_planes[:, g, :],
                            start=(g == 0),
                            stop=(g == PASSES - 1),
                        )
            for c in range(2 * PAIR):
                if hp == 0 and c < 2:
                    nc.scalar.copy(out=whole[s][:, c, EDGE * s : EDGE * s + PIXELS], in_=banks[c][:])
                    if s == 1:
                        nc.scalar.copy(out=whole[1][:, c, 0:EDGE], in_=banks[c][:, PIXELS - EDGE : PIXELS])
                elif s == 0:
                    split([q[hp][:, a, c, :] for a in range(2)], banks[c][:])
                else:
                    store_k(hp, c, banks[c][:], banks[c][:, PIXELS - EDGE : PIXELS])

        def project_head(hp, s, i):
            bank = ps_proj.tile([P, 2, PIXELS], F32, tag="proj")
            for c in range(2):
                lo = HEAD_DIM * i + P * c
                plane_lo = (hp % 2) * PAIR_DIM + lo
                for g in range(PASSES):
                    nc.tensor.matmul_mx(
                        out=bank[:, c, :],
                        lhsT=w_words[hp % 2][s][:, g, lo : lo + P].bitcast(FP8X4),
                        lhsT_scale=w_planes[s][hp // 2][plane_rows(g), plane_slot(g), plane_lo : plane_lo + P],
                        rhs=x_words[:, g, :].bitcast(FP8X4),
                        rhs_scale=x_planes[:, g, :],
                        start=(g == 0),
                        stop=(g == PASSES - 1),
                    )
            chans = slice(2 * i, 2 * i + 2)
            if s == 0:
                split([q[hp][:, a, chans, :] for a in range(2)], bank[:])
            else:
                store_k(hp, chans, bank[:], bank[:, :, PIXELS - EDGE : PIXELS])

        def project_tile(hp, t):
            plane_cols = slice((hp % 2) * PAIR_DIM, (hp % 2 + 1) * PAIR_DIM)
            bank = ps_proj.tile([P, PAIR_DIM], F32, name="v_bank", tag="proj")
            pix = slice(P * t, P * (t + 1))
            for g in range(PASSES):
                nc.tensor.matmul_mx(
                    out=bank[:],
                    lhsT=x_words[:, g, pix].bitcast(FP8X4),
                    lhsT_scale=x_planes[:, g, pix],
                    rhs=w_words[hp % 2][2][:, g, :].bitcast(FP8X4),
                    rhs_scale=w_planes[2][hp // 2][plane_rows(g), plane_slot(g), plane_cols],
                    start=(g == 0),
                    stop=(g == PASSES - 1),
                )
            split([v[hp][:, a, t, :] for a in range(2)], bank[:])

        def scores(hp, i):
            score = ps_att.tile([P, TILES, BAND], F32, tag="att")
            for t in range(TILES):
                pix = slice(P * t, P * (t + 1))
                if hp == 0 and i == 0:
                    terms = [(whole[0][:, c, pix], whole[1][:, c, band(t)]) for c in range(2)]
                else:
                    terms = [
                        (q[hp][:, a, 2 * i + c, pix], k[hp][:, b, 2 * i + c, band(t)])
                        for a, b in PRODUCTS
                        for c in range(2)
                    ]
                for n, (lhs, rhs) in enumerate(terms):
                    nc.tensor.matmul(
                        out=score[:, t, :], lhsT=lhs, rhs=rhs, start=(n == 0), stop=(n == len(terms) - 1)
                    )
            nc.vector.tensor_tensor(out=masked[i][:, :, 0:BAND], in0=score[:], in1=cap[:], op=ALU.min)
            neg_max = small.tile([P, TILES], F32, tag="neg_max")
            nc.vector.tensor_reduce(
                out=neg_max[:], in_=masked[i][:], axis=AXIS.X, op=ALU.max, negate=True
            )
            return neg_max

        def exponentials(i, neg_max):
            total = small.tile([P, TILES], F32, tag="total")
            exps = work.tile([P, TILES, BAND + OUTSIDE], F32, tag="exps")
            for t in range(TILES):
                nc.scalar.activation(
                    out=exps[:, t, :],
                    in_=masked[i][:, t, :],
                    func=FUNC.Exp,
                    bias=neg_max[:, t : t + 1],
                    scale=1.0,
                    accum_out=total[:, t : t + 1],
                )
            return exps, total

        def normalise(i, exps, total):
            inv_total = small.tile([P, TILES], F32, tag="inv_total")
            nc.vector.reciprocal(out=inv_total[:], in_=total[:])
            for t in range(TILES):
                nc.vector.tensor_scalar(
                    out=att[i][:, t, :],
                    in0=exps[:, t, 0:BAND],
                    scalar1=inv_total[:, t : t + 1],
                    scalar2=None,
                    op0=ALU.mult,
                )

        edges = {}

        def turn_edges(i):
            edges[i] = work.tile([P, TILES, EDGE], F32, name="edge_%d" % i, tag="edge_%d" % i, align_bytes=64)
            for t in range(TILES):
                nc.vector.transpose(out=edges[i][:, 1 - t, :], in_=att[i][:, t, 0:EDGE])

        def turn_tiles(hp, i):
            bank = ps_att.tile([P, TILES, P], F32, name="own", tag="att")
            for t in range(TILES):
                nc.tensor.transpose(out=bank[:, t, :], in_=att[i][:, t, EDGE:BAND], identity=ident[:])
            att_t[(hp, i)] = work.tile([P, 2, TILES, BAND], BF16, name="att_t_%d" % i, tag="att_t_%d" % i)
            split(
                [att_t[(hp, i)][:, a, :, EDGE:BAND] for a in range(2)], bank[:],
                [att_t[(hp, i)][:, a, :, 0:EDGE] for a in range(2)], edges[i][:],
            )

        def weighted_sum(hp):
            res = [results.tile([P, 2, PIXELS], F32, name="res_%d" % i, tag="res") for i in range(PAIR)]
            for i in range(PAIR):
                head = PAIR * hp + i
                steps = ((0, 0, 2), (1, 0, 2)) if head < HEADS - 1 else ((0, 0, 2), (1, 0, 1), (1, 1, 2))
                for j, lo, hi in steps:
                    part = ps_att.tile([P, hi - lo, BAND], F32, name="part", tag="att")
                    for c in range(lo, hi):
                        chan = slice(HEAD_DIM * i + P * c, HEAD_DIM * i + P * (c + 1))
                        for n, (a, b) in enumerate(PRODUCTS):
                            nc.tensor.matmul(
                                out=part[:, c - lo, :],
                                lhsT=v[hp][:, a, j, chan],
                                rhs=att_t[(hp, i)][:, b, j, :],
                                start=(n == 0),
                                stop=(n == len(PRODUCTS) - 1),
                            )
                    dest = res[i][:, lo:hi, :]
                    if j == 0:
                        nc.scalar.copy(out=dest[:, :, P : P + EDGE], in_=part[:, :, 0:EDGE])
                        nc.vector.tensor_copy(out=dest[:, :, 0:P], in_=part[:, :, EDGE:BAND])
                    else:
                        nc.scalar.copy(out=dest[:, :, P + EDGE : PIXELS], in_=part[:, :, EDGE:P])
                        both = dest[:, :, P - EDGE : P + EDGE].rearrange("p c (s w) -> p c s w", w=EDGE)
                        runs = part[:].rearrange("p c (s w) -> p c s w", w=EDGE)
                        ends = runs[:, :, 0 : BAND // EDGE : BAND // EDGE - 1, :]
                        nc.vector.tensor_tensor(out=both, in0=both, in1=ends, op=ALU.add)
                        nc.sync.dma_start(out=out_rows[:, 2 * head + lo : 2 * head + hi, :], in_=dest)

        def attend(hp):
            neg_max = [scores(hp, i) for i in range(PAIR)]
            return [exponentials(i, neg_max[i]) for i in range(PAIR)]

        def finish(exps):
            for i in range(PAIR):
                normalise(i, exps[i][0], exps[i][1])
            for i in range(PAIR):
                turn_edges(i)

        def project(hp, s):
            if s == 0:
                q[hp] = qkv.tile([P, 2, 2 * PAIR, PIXELS], BF16, name="q_halves", tag="q")
            elif s == 1:
                k[hp] = qkv.tile([P, 2, 2 * PAIR, EDGE + PIXELS], BF16, name="k_halves", tag="k")
            else:
                v[hp] = qkv.tile([P, 2, TILES, PAIR_DIM], BF16, name="v_halves", tag="v")
            if (hp, s) in IN_HALVES:
                project_in_halves(hp, s)
            elif s < 2:
                for i in range(PAIR):
                    project_head(hp, s, i)
            else:
                for t in range(TILES):
                    project_tile(hp, t)

        def turn(hp):
            for i in range(PAIR):
                turn_tiles(hp, i)

        project(0, 0)
        project(0, 1)
        finish(attend(0))
        project(1, 0)
        project(1, 1)
        turn(0)
        exps = attend(1)
        project(0, 2)
        finish(exps)
        load_scales(0, 1, 0, 6)
        load_words(2, 0)
        load_scales(0, 1, 6, SCALE_DMAS)
        load_scales(1, 1, 0, 4)
        load_words(2, 1)
        load_scales(1, 1, 4, SCALE_DMAS)
        project(1, 2)
        load_words(3, 0)
        load_scales(2, 1, 0, 4)
        load_words(3, 1)
        load_scales(2, 1, 4, SCALE_DMAS)
        load_words(2, 2)
        load_words(3, 2)
        turn(1)
        weighted_sum(0)
        weighted_sum(1)

        project(2, 0)
        project(2, 1)
        project(3, 0)
        finish(attend(2))
        project(3, 1)
        turn(2)
        exps = attend(3)
        project(2, 2)
        finish(exps)
        project(3, 2)
        turn(3)
        weighted_sum(2)
        weighted_sum(3)


def quantise_x(nc, x_grouped, x_words, x_planes, g):
    nc.vector.quantize_mx(
        out=x_words[:, g, :].bitcast(FP8X4),
        scales=x_planes[:, g, :],
        in_=x_grouped[:, g].rearrange("p n t -> p (n t)"),
    )


def build_mask(nc, pool, cap, masked):
    pix = pool.tile([P, TILES], I32)
    for t in range(TILES):
        nc.gpsimd.iota(pix[:, t : t + 1], pattern=[[0, 1]], base=EDGE * t, channel_multiplier=1)
    key_col = pool.tile([P, SIDE], F32)
    nc.gpsimd.iota(
        key_col[:], pattern=[[1, SIDE]], base=0, channel_multiplier=0, allow_small_or_imprecise_dtypes=True
    )
    key_row = pool.tile([P, TILES, BAND_ROWS], F32)
    for t in range(TILES):
        lo = 0
        for row, count in KEY_ROWS[t]:
            nc.gpsimd.iota(
                key_row[:, t, lo : lo + count], pattern=[[1, count]], base=row - TILE_ROWS * t,
                channel_multiplier=0, allow_small_or_imprecise_dtypes=True,
            )
            lo += count
    slot = pool.tile([P, OUTSIDE], F32)
    nc.gpsimd.iota(
        slot[:], pattern=[[1, OUTSIDE]], base=0, channel_multiplier=0, allow_small_or_imprecise_dtypes=True
    )
    row = pool.tile([P, TILES], I32)
    nc.vector.tensor_single_scalar(out=row[:], in_=pix[:], scalar=4, op=ALU.arith_shift_right)
    col = pool.tile([P, 1], I32)
    nc.vector.tensor_single_scalar(out=col[:], in_=pix[:, 0:1], scalar=SIDE - 1, op=ALU.bitwise_and)
    nc.vector.tensor_single_scalar(out=row[:], in_=row[:], scalar=TILE_ROWS - 1, op=ALU.bitwise_and)
    neg_col = pool.tile([P, 1], F32)
    nc.vector.tensor_scalar(out=neg_col[:], in0=col[:], scalar1=-1.0, scalar2=None, op0=ALU.mult)
    neg_row = pool.tile([P, TILES], F32)
    nc.vector.tensor_scalar(out=neg_row[:], in0=row[:], scalar1=-1.0, scalar2=None, op0=ALU.mult)
    col_dist = pool.tile([P, SIDE], F32)
    nc.vector.tensor_scalar(
        out=col_dist[:], in0=key_col[:], scalar1=neg_col[:, 0:1], scalar2=None, op0=ALU.add
    )
    row_dist = pool.tile([P, TILES, BAND_ROWS], F32)
    for t in range(TILES):
        nc.vector.tensor_scalar(
            out=row_dist[:, t, :], in0=key_row[:, t, :], scalar1=neg_row[:, t : t + 1], scalar2=None,
            op0=ALU.add,
        )
    squares, inside, caps = [], [], []
    axes = (("col", [P, 1, SIDE], col_dist[:]), ("row", [P, TILES * BAND_ROWS, 1], row_dist[:].rearrange("p t r -> p (t r)")))
    for name, shape, dist in axes:
        squares.append(pool.tile([P, shape[1] * shape[2]], F32, name="square_" + name))
        nc.vector.tensor_tensor(out=squares[-1][:], in0=dist, in1=dist, op=ALU.mult)
    for n, (name, shape, dist) in enumerate(axes):
        inside.append(pool.tile([P, shape[1] * shape[2]], F32, name="inside_" + name))
        nc.vector.tensor_scalar(
            out=inside[n][:], in0=squares[n][:], scalar1=REACH * REACH + 0.5, scalar2=None, op0=ALU.is_le
        )
    for n, (name, shape, dist) in enumerate(axes):
        caps.append(pool.tile(shape, F32, name="cap_" + name))
        nc.vector.tensor_scalar(
            out=caps[n][:].rearrange("p a b -> p (a b)"), in0=inside[n][:], scalar1=2.0 * BIG, scalar2=-BIG,
            op0=ALU.mult, op1=ALU.add,
        )
    cols = pool.tile([P, 1], F32)
    nc.vector.tensor_reduce(out=cols[:], in_=inside[0][:], axis=AXIS.X, op=ALU.add)
    rows = pool.tile([P, TILES], F32)
    nc.vector.tensor_reduce(
        out=rows[:], in_=inside[1][:].rearrange("p (t r) -> p t r", t=TILES), axis=AXIS.X, op=ALU.add
    )
    whole = [P, TILES * BAND_ROWS, SIDE]
    nc.vector.tensor_tensor(
        out=cap[:].rearrange("p t (r c) -> p (t r) c", c=SIDE),
        in0=caps[1][:].to_broadcast(whole), in1=caps[0][:].to_broadcast(whole), op=ALU.min,
    )
    count = pool.tile([P, TILES], F32)
    nc.vector.tensor_scalar(out=count[:], in0=rows[:], scalar1=cols[:, 0:1], scalar2=None, op0=ALU.mult)
    unused = pool.tile([P, TILES, OUTSIDE], F32)
    for t in range(TILES):
        nc.vector.tensor_scalar(
            out=unused[:, t, :], in0=slot[:], scalar1=count[:, t : t + 1], scalar2=WINDOW - 0.5,
            op0=ALU.add, op1=ALU.is_gt,
        )
    for tile_i in masked:
        nc.vector.tensor_scalar(
            out=tile_i[:, :, BAND : BAND + OUTSIDE], in0=unused[:], scalar1=-BIG, scalar2=None,
            op0=ALU.mult,
        )
